import numpy as np
import ml_dtypes


def mxq(x, axis, fmt="e4m3"):
    dtype, down = {"e4m3": (ml_dtypes.float8_e4m3fn, 7), "e5m2": (ml_dtypes.float8_e5m2, 14)}[fmt]
    v = np.moveaxis(np.asarray(x, np.float32).astype(ml_dtypes.bfloat16).astype(np.float64), axis, -1)
    blocks = v.reshape(v.shape[:-1] + (-1, 32))
    amax = np.abs(blocks).max(-1, keepdims=True)
    byte = np.maximum(np.where(amax > 0, np.frexp(amax)[1] - 1 + 127, 0) - down, 1)
    scale = np.exp2(byte - 127.0)
    codes = (blocks / scale).astype(np.float32).astype(dtype).astype(np.float64)
    return np.moveaxis((codes * scale).reshape(v.shape), -1, axis)


WIDE = False


def mx_kscale(k):
    if not WIDE:
        return np.ones(k)
    levels = np.array([10, -10, 5, -5, 0])
    if k % 512:
        return np.exp2(np.random.permutation(np.resize(levels, k // 32))).repeat(32)
    a = np.empty((k // 512, 16))
    for p in range(k // 512):
        a[p, :8] = np.random.permutation(np.resize(levels, 8))
        for g in range(8):
            far = levels[np.abs(levels - a[p, g]) >= 10]
            a[p, g + 8] = far[np.random.randint(len(far))]
    return np.exp2(a.ravel()).repeat(32)


BF16 = ml_dtypes.bfloat16


def bf(x):
    return np.asarray(x, np.float32).astype(BF16)


def f64(x):
    return np.asarray(x).astype(np.float64)


E2M1 = np.array([0.0, 0.5, 1.0, 1.5, 2.0, 3.0, 4.0, 6.0, -0.0, -0.5, -1.0, -1.5, -2.0, -3.0, -4.0, -6.0])


def pack_weight(w, fmt):
    k, n = w.shape
    w = f64(bf(w)).reshape(k // 32, 32, n)
    amax = np.abs(w).max(1)
    if fmt == "e4m3":
        byte = np.frexp(amax)[1] - 1 + 127 - 7
    else:
        mant, ex = np.frexp(amax / 6.0)
        byte = np.where(mant > 0.5, ex, ex - 1) + 127
    byte = np.clip(np.where(amax > 0, byte, 1), 1, 254)
    scaled = (w * np.exp2(127.0 - byte)[:, None, :]).reshape(k, n).astype(np.float32)
    by_word = np.ascontiguousarray(scaled.reshape(k // 512, 128, 4, n).transpose(0, 1, 3, 2))
    if fmt == "e4m3":
        words = by_word.astype(ml_dtypes.float8_e4m3fn).view(np.uint8)
    else:
        c = by_word.astype(ml_dtypes.float4_e2m1fn).view(np.uint8) & 0xF
        words = c[..., 0::2] | (c[..., 1::2] << 4)
    return np.ascontiguousarray(words), np.ascontiguousarray(byte.astype(np.uint8).reshape(k // 512, 16, n))


def unpack_weight(words, scales, fmt):
    g, p, n, _ = words.shape
    if fmt == "e4m3":
        vals = np.ascontiguousarray(words).view(ml_dtypes.float8_e4m3fn).astype(np.float64)
    else:
        nib = np.empty((g, p, n, 4), np.uint8)
        nib[..., 0::2] = words & 0xF
        nib[..., 1::2] = words >> 4
        vals = E2M1[nib]
    vals = vals * np.repeat(np.exp2(scales.astype(np.float64) - 127.0), 8, axis=1)[..., None]
    return vals.transpose(0, 1, 3, 2).reshape(g * 512, n)


B, K_SLOTS, P, SLOT, HID, NC, NP = 256, 8, 1536, 512, 512, 512, 512
KEY_SCALE = 3.0


def softmax(z):
    e = np.exp(z - z.max(-1, keepdims=True))
    return e / e.sum(-1, keepdims=True)


def draw0():
    rn = np.random.standard_normal
    s, t = mx_kscale(P), mx_kscale(P)
    inst_embed = bf(rn((B, P)) * s)
    Wfc_words, Wfc_scales = pack_weight(rn((P, P)) / np.sqrt(P) / s[:, None] * t, "e4m3")
    bfc = bf(0.3 * rn(P) * t)
    Wfp_words, Wfp_scales = pack_weight(rn((P, P)) / np.sqrt(P) / s[:, None] * t, "e4m3")
    bfp = bf(0.3 * rn(P) * t)
    Kc_words, Kc_scales = pack_weight((KEY_SCALE * rn((NC, P)) / t).T, "e4m3")
    Kp_words, Kp_scales = pack_weight((KEY_SCALE * rn((NP, P)) / t).T, "e4m3")
    return {"inst_embed": inst_embed,
            "Wfc_words": Wfc_words, "Wfc_scales": Wfc_scales, "bfc": bfc,
            "Wfp_words": Wfp_words, "Wfp_scales": Wfp_scales, "bfp": bfp,
            "Kc_words": Kc_words, "Kc_scales": Kc_scales,
            "Kp_words": Kp_words, "Kp_scales": Kp_scales}


def core(inst_embed, Wfc_words, Wfc_scales, bfc, Wfp_words, Wfp_scales, bfp, Kc_words, Kc_scales, Kp_words, Kp_scales):
    xq = mxq(f64(inst_embed), 1, "e4m3")
    Qc = (xq @ unpack_weight(Wfc_words, Wfc_scales, "e4m3")) + f64(bfc)
    Qp = (xq @ unpack_weight(Wfp_words, Wfp_scales, "e4m3")) + f64(bfp)
    zc = (mxq(Qc, 1, "e4m3") @ unpack_weight(Kc_words, Kc_scales, "e4m3")) / np.sqrt(P)
    zp = (mxq(Qp, 1, "e4m3") @ unpack_weight(Kp_words, Kp_scales, "e4m3")) / np.sqrt(P)
    return softmax(zc), softmax(zp)


def e4m3fn_bytes(y):
    return np.clip(np.asarray(y, np.float64), -448.0, 448.0).astype(np.float32).astype(ml_dtypes.float8_e4m3fn).view(np.uint8)


def e4m3fn_values(b):
    return np.asarray(b, np.uint8).view(ml_dtypes.float8_e4m3fn).astype(np.float64)


def setup_inputs():
    d = draw0()
    x0 = np.asarray(d['inst_embed']).astype(np.float64)
    s = (np.max(np.abs(x0), axis=(0,), keepdims=True) / 448.0).astype(np.float32)
    out = {}
    for k, v in d.items():
        if k == 'inst_embed':
            out['inst_embed_bytes'] = e4m3fn_bytes(x0 / s.astype(np.float64))
            out['inst_embed_scale'] = s
        else:
            out[k] = v
    return out


def reference(inst_embed_bytes, inst_embed_scale, Wfc_words, Wfc_scales, bfc, Wfp_words, Wfp_scales, bfp, Kc_words, Kc_scales, Kp_words, Kp_scales):
    return core(e4m3fn_values(inst_embed_bytes) * inst_embed_scale.astype(np.float64), Wfc_words, Wfc_scales, bfc, Wfp_words, Wfp_scales, bfp, Kc_words, Kc_scales, Kp_words, Kp_scales)

@@ -1,0 +1,374 @@
+from contextlib import ExitStack
+
+import concourse.mybir as mybir
+from concourse.masks import make_identity
+
+F32 = mybir.dt.float32
+BF16 = mybir.dt.bfloat16
+U32 = mybir.dt.uint32
+I32 = mybir.dt.int32
+U8 = mybir.dt.uint8
+FP8 = mybir.dt.float8_e4m3fn
+FP8X4 = mybir.dt.float8_e4m3fn_x4
+ALU = mybir.AluOpType
+ACT = mybir.ActivationFunctionType
+AXIS = mybir.AxisListType
+
+TOKENS, WIDTH, KEYS = 256, 1536, 512
+P = 128
+GROUP = 512
+GROUPS = WIDTH // GROUP
+HALVES = TOKENS // P
+FLOPS = 2 * (2 * TOKENS * WIDTH * WIDTH + 2 * TOKENS * WIDTH * KEYS)
+WARM = 5
+AWAY = {(0, 1, 1), (0, 2, 1)}
+INV_SQRT = 1.0 / WIDTH**0.5
+
+
+def tile_executor_pa_w8_kernel(
+    tc, x_bytes, x_scale, wc_words, wc_scales, bc, wp_words, wp_scales, bp, kc_words, kc_scales, kp_words, kp_scales, out_c, out_p
+):
+    nc = tc.nc
+    with ExitStack() as ctx:
+        keep = ctx.enter_context(tc.tile_pool(name="keep", bufs=1))
+        psum = ctx.enter_context(tc.psum_pool(name="psum", bufs=1))
+        ctx.enter_context(tc.manual_schedule())
+
+        def sb(name, shape, dtype):
+            return keep.tile(shape, dtype, name=name, tag=name, align_bytes=256)
+
+        def bank(name, which, shape, dtype):
+            return psum.tile(shape, dtype, name=name, tag="bank%d" % which)
+
+        x8_head = sb("x8_head", [P, HALVES, GROUP], U8)
+        x8_rest = sb("x8_rest", [P, HALVES, WIDTH - GROUP], U8)
+        xw = [sb("xw_%d" % g, [P, HALVES, GROUP], BF16) for g in range(GROUPS)]
+        xs = sb("xs", [P, GROUPS, 4], F32)
+        xg = [sb("xg_%d" % g, [P, HALVES, P, 4], BF16) for g in range(GROUPS)]
+        xq = [sb("xq_%d" % g, [P, TOKENS], U32) for g in range(GROUPS)]
+        xqs = [sb("xqs_%d" % g, [P, TOKENS], U8) for g in range(GROUPS)]
+        wc = [[sb("wc_%d_%d" % (g, n), [P, GROUP], U32) for n in range(GROUPS)] if g == 0 else sb("wc_%d" % g, [P, WIDTH], U32) for g in range(GROUPS)]
+        wp = [sb("wp_%d" % n, [P, GROUPS, GROUP], U32) for n in range(GROUPS)]
+        kc = sb("kc", [P, GROUPS, KEYS], U32)
+        kp = sb("kp", [P, GROUPS, KEYS], U32)
+        wcs = sb("wcs", [P, GROUPS, WIDTH], U8)
+        wps = sb("wps", [P, GROUPS, WIDTH], U8)
+        kcs = sb("kcs", [P, GROUPS, KEYS], U8)
+        kps = sb("kps", [P, GROUPS, KEYS], U8)
+        ident = sb("ident", [P, P], F32)
+        ones = sb("ones", [P, P], BF16)
+        brow = [sb("brow_%d" % q, [P, WIDTH], BF16) for q in range(2)]
+        bias = [sb("bias_%d" % q, [P, WIDTH], BF16) for q in range(2)]
+        qb = [[[sb("qb_%d_%d_%d" % (q, n, t), [P, GROUP], BF16) for t in range(HALVES)] for n in range(GROUPS)] for q in range(2)]
+        qt = [[sb("qt_%d_%d" % (q, n), [P, TOKENS, 2], F32) for n in range(GROUPS)] for q in range(2)]
+        qq = [[sb("qq_%d_%d" % (q, n), [P, TOKENS], U32) for n in range(GROUPS)] for q in range(2)]
+        qqs = [[sb("qqs_%d_%d" % (q, n), [P, TOKENS], U8) for n in range(GROUPS)] for q in range(2)]
+        warm = sb("warm", [P, 1], F32)
+        zeros = sb("zeros", [P, GROUP], BF16)
+
+        xv = x_bytes.rearrange("(t p) k -> p t k", t=HALVES)
+
+        def scales_in(dst, src, quads=range(4)):
+            for q in quads:
+                nc.sync.dma_start(
+                    out=dst[32 * q : 32 * q + 4, :, :].bitcast(I32),
+                    in_=src[:, 4 * q : 4 * q + 4, :].rearrange("g r n -> r g n").bitcast(I32),
+                )
+
+        def clear(engine, t):
+            engine.memset(t.bitcast(I32), 0)
+
+        def flat(t):
+            return t[:].rearrange("p g n -> p (g n)")
+
+        def load_wc(g, n=None):
+            src = wc_words[g].rearrange("p n t -> p (n t)")
+            if n is None:
+                nc.sync.dma_start(out=wc[g][:].bitcast(I32), in_=src.bitcast(I32))
+            else:
+                nc.sync.dma_start(out=wc[g][n][:].bitcast(I32), in_=src[:, 4 * n * GROUP : 4 * (n + 1) * GROUP].bitcast(I32))
+
+        nc.sync.dma_start(out=x8_head[:], in_=xv[:, :, 0:GROUP])
+        clear(nc.vector, brow[0][:])
+        nc.sync.dma_start(out=brow[0][0:1, :], in_=bc.rearrange("(o n) -> o n", o=1))
+        nc.sync.dma_start(out=x8_rest[:], in_=xv[:, :, GROUP:WIDTH])
+        nc.vector.memset(ones[:], 0.0)
+        nc.vector.memset(ones[0:1, :], 1.0)
+        clear(nc.vector, zeros[:])
+        clear(nc.vector, brow[1][:])
+        nc.vector.memset(warm[:], 0.0)
+        nc.scalar.activation(warm[:], warm[:], ACT.Exp)
+        clear(nc.gpsimd, flat(wcs))
+        nc.gpsimd.dma_start(out=xs[:], in_=x_scale.rearrange("o (g p t) -> p (o g) t", p=P, t=4))
+        make_identity(nc, ident[:])
+        clear(nc.gpsimd, flat(wps))
+        clear(nc.gpsimd, flat(kcs))
+        clear(nc.gpsimd, flat(kps))
+        load_wc(0, 0)
+        nc.sync.dma_start(out=brow[1][0:1, :], in_=bp.rearrange("(o n) -> o n", o=1))
+        scales_in(wcs, wc_scales)
+        load_wc(0, 1)
+        load_wc(0, 2)
+        load_wc(1)
+        load_wc(2)
+        scales_in(wps, wp_scales)
+
+        def load_wp(n):
+            nc.sync.dma_start(
+                out=wp[n][:].bitcast(I32),
+                in_=wp_words[:, :, n * GROUP : (n + 1) * GROUP, :].rearrange("g p n t -> p g (n t)").bitcast(I32),
+            )
+
+        load_wp(0)
+        scales_in(kcs, kc_scales)
+        load_wp(1)
+        scales_in(kps, kp_scales)
+        load_wp(2)
+        nc.sync.dma_start(out=kc[:].bitcast(I32), in_=kc_words.rearrange("g p n t -> p g (n t)").bitcast(I32))
+        nc.sync.dma_start(out=kp[:].bitcast(I32), in_=kp_words.rearrange("g p n t -> p g (n t)").bitcast(I32))
+
+        def widen(engine_copy, g, t):
+            engine_copy(out=xw[g][:, t, :], in_=(x8_head[:, t, :] if g == 0 else x8_rest[:, t, (g - 1) * GROUP : g * GROUP]).bitcast(FP8))
+
+        def x_transposes(g, b):
+            xt = bank("xt_%d" % g, b, [P, 2, HALVES, P], F32)
+            for t in range(HALVES):
+                words = xw[g][:, t, :].bitcast(F32)
+                for u in range(2):
+                    nc.tensor.transpose(xt[:, u, t, :], words[:, u : GROUP // 2 : 2], ident[:])
+            return xt
+
+        def x_scaled(xt, g, t):
+            nc.vector.tensor_tensor(
+                out=xg[g][:, t, :, :].rearrange("p r (u e) -> p r u e", e=2),
+                in0=xt[:, :, t, :].bitcast(BF16).rearrange("p u (r e) -> p r u e", e=2),
+                in1=xs[:, g : g + 1, :].to_broadcast([P, P, 4]).rearrange("p r (u e) -> p r u e", e=2),
+                op=ALU.mult,
+            )
+
+        def x_scaled_whole(xt, g):
+            nc.vector.tensor_tensor(
+                out=xg[g][:].rearrange("p t r (u e) -> p (t r) u e", e=2),
+                in0=xt[:].rearrange("p u t r -> p u (t r)").bitcast(BF16).rearrange("p u (r e) -> p r u e", e=2),
+                in1=xs[:, g : g + 1, :].to_broadcast([P, TOKENS, 4]).rearrange("p r (u e) -> p r u e", e=2),
+                op=ALU.mult,
+            )
+
+        def x_quantize_whole(g):
+            nc.vector.quantize_mx(out=xq[g][:].bitcast(FP8X4), scales=xqs[g][:], in_=xg[g][:].rearrange("p t r j -> p (t r j)"))
+
+        def x_quantize(g, t):
+            cols = slice(t * P, (t + 1) * P)
+            nc.vector.quantize_mx(
+                out=xq[g][:, cols].bitcast(FP8X4), scales=xqs[g][:, cols], in_=xg[g][:, t, :, :].rearrange("p r j -> p (r j)")
+            )
+
+        def pass_c(acc, g, n, t):
+            rows = slice(t * P, (t + 1) * P)
+            cols = slice(n * GROUP, (n + 1) * GROUP)
+            nc.tensor.matmul_mx(
+                out=acc[:], lhsT=xq[g][:, rows].bitcast(FP8X4), lhsT_scale=xqs[g][:, rows],
+                rhs=(wc[g][n][:] if g == 0 else wc[g][:, cols]).bitcast(FP8X4), rhs_scale=wcs[:, g, cols], start=(g == 0), stop=(g == GROUPS - 1),
+            )
+
+        def pass_p(acc, g, n, t):
+            rows = slice(t * P, (t + 1) * P)
+            cols = slice(n * GROUP, (n + 1) * GROUP)
+            nc.tensor.matmul_mx(
+                out=acc[:], lhsT=xq[g][:, rows].bitcast(FP8X4), lhsT_scale=xqs[g][:, rows],
+                rhs=wp[n][:, g, :].bitcast(FP8X4), rhs_scale=wps[:, g, cols], start=(g == 0), stop=(g == GROUPS - 1),
+            )
+
+        def add_bias(acc, q, n, t):
+            if (q, n, t) in AWAY:
+                side = sb("side_%d_%d_%d" % (q, n, t), [P, GROUP], F32)
+                nc.scalar.copy(out=side[:], in_=acc[:])
+                acc = side
+                engine = nc.gpsimd
+            else:
+                engine = nc.vector
+            engine.tensor_tensor(
+                out=qb[q][n][t][:].rearrange("p (u m e) -> p u m e", u=2, e=2),
+                in0=acc[:].rearrange("p (m u e) -> p u m e", u=2, e=2),
+                in1=bias[q][:, n * GROUP : (n + 1) * GROUP].rearrange("p (u m e) -> p u m e", u=2, e=2),
+                op=ALU.add,
+            )
+
+        def bias_bank(name, b):
+            return bank(name, b, [P, 2, GROUP], BF16)
+
+        def spread_bias(bt, slot, q, n):
+            nc.tensor.matmul(bt[:, slot, :], ones[:], brow[q][:, n * GROUP : (n + 1) * GROUP], start=True, stop=True)
+
+        def keep_bias(bt, slot, q, n):
+            nc.scalar.copy(
+                out=bias[q][:, n * GROUP : (n + 1) * GROUP].rearrange("p (u m e) -> p u m e", u=2, e=2),
+                in_=bt[:, slot, :].rearrange("p (m u e) -> p u m e", u=2, e=2),
+            )
+
+        def q_transposes(q, n, b):
+            tb = bank("tb_%d_%d" % (q, n), b, [P, 2, TOKENS], F32)
+            for t in range(HALVES):
+                words = qb[q][n][t][:].bitcast(F32)
+                for u in range(2):
+                    nc.tensor.transpose(tb[:, u, t * P : (t + 1) * P], words[:, u * P : (u + 1) * P], ident[:])
+            return tb
+
+        def q_empty(tb, q, n):
+            nc.scalar.copy(out=qt[q][n][:], in_=tb[:].rearrange("p u r -> p r u"))
+
+        def q_empty_half(tb, q, n, t):
+            rows = slice(t * P, (t + 1) * P)
+            nc.scalar.copy(out=qt[q][n][:, rows, :], in_=tb[:, :, rows].rearrange("p u r -> p r u"))
+
+        def q_quantize_half(q, n, t):
+            rows = slice(t * P, (t + 1) * P)
+            nc.vector.quantize_mx(
+                out=qq[q][n][:, rows].bitcast(FP8X4),
+                scales=qqs[q][n][:, rows],
+                in_=qt[q][n][:, rows, :].rearrange("p r u -> p (r u)").bitcast(BF16),
+            )
+
+        def q_quantize(q, n):
+            nc.vector.quantize_mx(
+                out=qq[q][n][:].bitcast(FP8X4), scales=qqs[q][n][:], in_=qt[q][n][:].rearrange("p r u -> p (r u)").bitcast(BF16)
+            )
+
+        def score(z, q, n, t):
+            rows = slice(t * P, (t + 1) * P)
+            k, ks = ((kc, kcs), (kp, kps))[q]
+            nc.tensor.matmul_mx(
+                out=z[:], lhsT=qq[q][n][:, rows].bitcast(FP8X4), lhsT_scale=qqs[q][n][:, rows],
+                rhs=k[:, n, :].bitcast(FP8X4), rhs_scale=ks[:, n, :], start=(n == 0), stop=(n == GROUPS - 1),
+            )
+
+        peak = [[sb("peak_%d_%d" % (q, t), [P, 1], F32) for t in range(HALVES)] for q in range(2)]
+        shift = [[sb("shift_%d_%d" % (q, t), [P, 1], F32) for t in range(HALVES)] for q in range(2)]
+        total = [[sb("total_%d_%d" % (q, t), [P, 1], F32) for t in range(HALVES)] for q in range(2)]
+        recip = [[sb("recip_%d_%d" % (q, t), [P, 1], F32) for t in range(HALVES)] for q in range(2)]
+        expo = [[sb("expo_%d_%d" % (q, t), [P, KEYS], F32) for t in range(HALVES)] for q in range(2)]
+        soft = [[sb("soft_%d_%d" % (q, t), [P, KEYS], F32) for t in range(HALVES)] for q in range(2)]
+
+        def row_max(z, q, t):
+            nc.vector.tensor_reduce(out=peak[q][t][:], in_=z[:], axis=AXIS.X, op=ALU.max)
+            nc.vector.tensor_scalar(out=shift[q][t][:], in0=peak[q][t][:], scalar1=-INV_SQRT, scalar2=None, op0=ALU.mult)
+
+        def row_exp(z, q, t):
+            nc.scalar.activation(expo[q][t][:], z[:], ACT.Exp, bias=shift[q][t][:], scale=INV_SQRT, accum_out=total[q][t][:])
+
+        def normalise(q, t, on_scalar):
+            nc.vector.reciprocal(out=recip[q][t][:], in_=total[q][t][:])
+            if on_scalar:
+                nc.gpsimd.tensor_scalar(out=soft[q][t][:], in0=expo[q][t][:], scalar1=recip[q][t][:], scalar2=0.0, op0=ALU.mult, op1=ALU.add)
+            else:
+                nc.vector.tensor_scalar(out=soft[q][t][:], in0=expo[q][t][:], scalar1=recip[q][t][:], scalar2=None, op0=ALU.mult)
+            nc.sync.dma_start(out=(out_c, out_p)[q][t * P : (t + 1) * P, :], in_=soft[q][t][:])
+
+        for i in range(WARM):
+            nc.tensor.matmul(bank("warm_%d" % i, 7, [P, GROUP], F32)[:], ones[:], zeros[:], start=True, stop=True)
+        widen(nc.vector.tensor_copy, 0, 0)
+        widen(nc.scalar.copy, 0, 1)
+        widen(nc.scalar.copy, 1, 0)
+        widen(nc.vector.tensor_copy, 2, 0)
+        widen(nc.scalar.copy, 1, 1)
+        widen(nc.scalar.copy, 2, 1)
+        xt0 = x_transposes(0, 0)
+        bt_c = bias_bank("bt_c", 4)
+        bt_t = bias_bank("bt_t", 6)
+        bt_p = bias_bank("bt_p", 2)
+        spread_bias(bt_t, 0, 0, 2)
+        for n in range(2):
+            spread_bias(bt_c, n, 0, n)
+        keep_bias(bt_t, 0, 0, 2)
+        for n in range(2):
+            keep_bias(bt_c, n, 0, n)
+        x_scaled(xt0, 0, 0)
+        x_quantize(0, 0)
+        x_scaled(xt0, 0, 1)
+        x_quantize(0, 1)
+        xt1 = x_transposes(1, 1)
+        x_scaled(xt1, 1, 0)
+        x_scaled(xt1, 1, 1)
+        x_quantize(1, 0)
+        acc_c = {}
+        for n in range(GROUPS):
+            acc_c[n, 0] = bank("acc_c_%d_0" % n, (3, 5, 7)[n], [P, GROUP], F32)
+        pass_c(acc_c[0, 0], 0, 0, 0)
+        for n in range(2):
+            spread_bias(bt_p, n, 1, n)
+            keep_bias(bt_p, n, 1, n)
+        for n in range(1, GROUPS):
+            pass_c(acc_c[n, 0], 0, n, 0)
+        xt2 = x_transposes(2, 0)
+        spread_bias(bt_t, 1, 1, 2)
+        keep_bias(bt_t, 1, 1, 2)
+        for n in range(GROUPS):
+            acc_c[n, 1] = bank("acc_c_%d_1" % n, (4, 6, 2)[n], [P, GROUP], F32)
+            pass_c(acc_c[n, 1], 0, n, 1)
+        x_scaled(xt2, 2, 0)
+        x_quantize(1, 1)
+        x_scaled(xt2, 2, 1)
+        x_quantize(2, 0)
+        x_quantize(2, 1)
+        for t in range(HALVES):
+            for n in range(GROUPS):
+                pass_c(acc_c[n, t], 1, n, t)
+        for n in range(GROUPS):
+            for t in range(HALVES):
+                pass_c(acc_c[n, t], 2, n, t)
+                add_bias(acc_c[n, t], 0, n, t)
+
+        def project_p(n, banks):
+            accs = []
+            for t in range(HALVES):
+                acc = bank("acc_p_%d_%d" % (n, t), banks[t], [P, GROUP], F32)
+                for g in range(GROUPS):
+                    pass_p(acc, g, n, t)
+                accs.append(acc)
+            return accs
+
+        acc = project_p(0, (1, 0))
+        q_empty(q_transposes(0, 0, 3), 0, 0)
+        q_empty(q_transposes(0, 1, 4), 0, 1)
+        for t in range(HALVES):
+            add_bias(acc[t], 1, 0, t)
+        q_quantize(0, 0)
+        q_quantize(0, 1)
+        acc = project_p(1, (5, 6))
+        q_empty(q_transposes(0, 2, 7), 0, 2)
+        q_empty(q_transposes(1, 0, 2), 1, 0)
+        for t in range(HALVES):
+            add_bias(acc[t], 1, 1, t)
+        q_quantize(0, 2)
+        q_quantize(1, 0)
+        zc = [bank("zc_%d" % t, (3, 4)[t], [P, KEYS], F32) for t in range(HALVES)]
+        acc = project_p(2, (1, 0))
+        for t in range(HALVES):
+            add_bias(acc[t], 1, 2, t)
+        for n in range(GROUPS):
+            score(zc[0], 0, n, 0)
+        tb = [q_transposes(1, n, (None, 5, 6)[n]) for n in (1, 2)]
+        q_empty(tb[0], 1, 1)
+        for t in range(HALVES):
+            q_empty_half(tb[1], 1, 2, t)
+        row_max(zc[0], 0, 0)
+        row_exp(zc[0], 0, 0)
+        for n in range(GROUPS):
+            score(zc[1], 0, n, 1)
+        q_quantize(1, 1)
+        for t in range(HALVES):
+            q_quantize_half(1, 2, t)
+        zp = [bank("zp_%d" % t, (7, 2)[t], [P, KEYS], F32) for t in range(HALVES)]
+        for t in range(HALVES):
+            for n in range(GROUPS):
+                score(zp[t], 1, n, t)
+        row_max(zc[1], 0, 1)
+        row_exp(zc[1], 0, 1)
+        normalise(0, 0, True)
+        row_max(zp[0], 1, 0)
+        row_exp(zp[0], 1, 0)
+        row_max(zp[1], 1, 1)
+        normalise(0, 1, True)
+        row_exp(zp[1], 1, 1)
+        normalise(1, 0, False)
+        normalise(1, 1, False)

@@ -20,7 +20,7 @@ GROUP = 512
 GROUPS = WIDTH // GROUP
 HALVES = TOKENS // P
 FLOPS = 2 * (2 * TOKENS * WIDTH * WIDTH + 2 * TOKENS * WIDTH * KEYS)
-WARM = 5
+WARM = 4
 AWAY = {(0, 1, 1), (0, 2, 1)}
 INV_SQRT = 1.0 / WIDTH**0.5
 
@@ -68,11 +68,11 @@ def tile_executor_pa_w8_kernel(
 
         xv = x_bytes.rearrange("(t p) k -> p t k", t=HALVES)
 
-        def scales_in(dst, src, quads=range(4)):
-            for q in quads:
+        def scales_in(dst, src, rows):
+            for r in rows:
                 nc.sync.dma_start(
-                    out=dst[32 * q : 32 * q + 4, :, :].bitcast(I32),
-                    in_=src[:, 4 * q : 4 * q + 4, :].rearrange("g r n -> r g n").bitcast(I32),
+                    out=dst[r:P:32, :, :].bitcast(I32),
+                    in_=src[:, r:16:4, :].rearrange("g q n -> q g n").bitcast(I32),
                 )
 
         def clear(engine, t):
@@ -89,29 +89,30 @@ def tile_executor_pa_w8_kernel(
                 nc.sync.dma_start(out=wc[g][n][:].bitcast(I32), in_=src[:, 4 * n * GROUP : 4 * (n + 1) * GROUP].bitcast(I32))
 
         nc.sync.dma_start(out=x8_head[:], in_=xv[:, :, 0:GROUP])
-        clear(nc.vector, brow[0][:])
-        nc.sync.dma_start(out=brow[0][0:1, :], in_=bc.rearrange("(o n) -> o n", o=1))
         nc.sync.dma_start(out=x8_rest[:], in_=xv[:, :, GROUP:WIDTH])
+        nc.gpsimd.dma_start(out=xs[:], in_=x_scale.rearrange("o (g p t) -> p (o g) t", p=P, t=4))
+        clear(nc.vector, flat(wcs))
+        scales_in(wcs, wc_scales, range(4))
+        clear(nc.vector, brow[0][:])
         nc.vector.memset(ones[:], 0.0)
-        nc.vector.memset(ones[0:1, :], 1.0)
         clear(nc.vector, zeros[:])
+        nc.vector.memset(ones[0:1, :], 1.0)
         clear(nc.vector, brow[1][:])
+        clear(nc.vector, flat(wps))
         nc.vector.memset(warm[:], 0.0)
         nc.scalar.activation(warm[:], warm[:], ACT.Exp)
-        clear(nc.gpsimd, flat(wcs))
-        nc.gpsimd.dma_start(out=xs[:], in_=x_scale.rearrange("o (g p t) -> p (o g) t", p=P, t=4))
         make_identity(nc, ident[:])
-        clear(nc.gpsimd, flat(wps))
         clear(nc.gpsimd, flat(kcs))
+        nc.gpsimd.dma_start(out=brow[0][0:1, :], in_=bc.rearrange("(o n) -> o n", o=1))
+        nc.gpsimd.dma_start(out=brow[1][0:1, :], in_=bp.rearrange("(o n) -> o n", o=1))
         clear(nc.gpsimd, flat(kps))
         load_wc(0, 0)
-        nc.sync.dma_start(out=brow[1][0:1, :], in_=bp.rearrange("(o n) -> o n", o=1))
-        scales_in(wcs, wc_scales)
         load_wc(0, 1)
         load_wc(0, 2)
         load_wc(1)
+        scales_in(wps, wp_scales, (0, 1))
         load_wc(2)
-        scales_in(wps, wp_scales)
+        scales_in(wps, wp_scales, (2, 3))
 
         def load_wp(n):
             nc.sync.dma_start(
@@ -120,11 +121,13 @@ def tile_executor_pa_w8_kernel(
             )
 
         load_wp(0)
-        scales_in(kcs, kc_scales)
+        scales_in(kcs, kc_scales, (0, 1))
         load_wp(1)
-        scales_in(kps, kp_scales)
+        scales_in(kcs, kc_scales, (2, 3))
         load_wp(2)
+        scales_in(kps, kp_scales, (0, 1))
         nc.sync.dma_start(out=kc[:].bitcast(I32), in_=kc_words.rearrange("g p n t -> p g (n t)").bitcast(I32))
+        scales_in(kps, kp_scales, (2, 3))
         nc.sync.dma_start(out=kp[:].bitcast(I32), in_=kp_words.rearrange("g p n t -> p g (n t)").bitcast(I32))
 
         def widen(engine_copy, g, t):
@@ -273,15 +276,6 @@ def tile_executor_pa_w8_kernel(
         widen(nc.scalar.copy, 1, 1)
         widen(nc.scalar.copy, 2, 1)
         xt0 = x_transposes(0, 0)
-        bt_c = bias_bank("bt_c", 4)
-        bt_t = bias_bank("bt_t", 6)
-        bt_p = bias_bank("bt_p", 2)
-        spread_bias(bt_t, 0, 0, 2)
-        for n in range(2):
-            spread_bias(bt_c, n, 0, n)
-        keep_bias(bt_t, 0, 0, 2)
-        for n in range(2):
-            keep_bias(bt_c, n, 0, n)
         x_scaled(xt0, 0, 0)
         x_quantize(0, 0)
         x_scaled(xt0, 0, 1)
@@ -293,15 +287,13 @@ def tile_executor_pa_w8_kernel(
         acc_c = {}
         for n in range(GROUPS):
             acc_c[n, 0] = bank("acc_c_%d_0" % n, (3, 5, 7)[n], [P, GROUP], F32)
-        pass_c(acc_c[0, 0], 0, 0, 0)
-        for n in range(2):
-            spread_bias(bt_p, n, 1, n)
-            keep_bias(bt_p, n, 1, n)
-        for n in range(1, GROUPS):
+        for n in range(GROUPS):
             pass_c(acc_c[n, 0], 0, n, 0)
         xt2 = x_transposes(2, 0)
-        spread_bias(bt_t, 1, 1, 2)
-        keep_bias(bt_t, 1, 1, 2)
+        bt_c = bias_bank("bt_c", 2)
+        for n in range(2):
+            spread_bias(bt_c, n, 0, n)
+            keep_bias(bt_c, n, 0, n)
         for n in range(GROUPS):
             acc_c[n, 1] = bank("acc_c_%d_1" % n, (4, 6, 2)[n], [P, GROUP], F32)
             pass_c(acc_c[n, 1], 0, n, 1)
@@ -310,9 +302,18 @@ def tile_executor_pa_w8_kernel(
         x_scaled(xt2, 2, 1)
         x_quantize(2, 0)
         x_quantize(2, 1)
-        for t in range(HALVES):
-            for n in range(GROUPS):
-                pass_c(acc_c[n, t], 1, n, t)
+        for n in range(GROUPS):
+            pass_c(acc_c[n, 0], 1, n, 0)
+        bt_t = bias_bank("bt_t", 1)
+        for q in range(2):
+            spread_bias(bt_t, q, q, 2)
+            keep_bias(bt_t, q, q, 2)
+        for n in range(GROUPS):
+            pass_c(acc_c[n, 1], 1, n, 1)
+        bt_p = bias_bank("bt_p", 0)
+        for n in range(2):
+            spread_bias(bt_p, n, 1, n)
+            keep_bias(bt_p, n, 1, n)
         for n in range(GROUPS):
             for t in range(HALVES):
                 pass_c(acc_c[n, t], 2, n, t)

@@ -12,7 +12,6 @@ FP8 = mybir.dt.float8_e4m3fn
 FP8X4 = mybir.dt.float8_e4m3fn_x4
 ALU = mybir.AluOpType
 ACT = mybir.ActivationFunctionType
-AXIS = mybir.AxisListType
 
 TOKENS, WIDTH, KEYS = 256, 1536, 512
 P = 128
@@ -20,8 +19,7 @@ GROUP = 512
 GROUPS = WIDTH // GROUP
 HALVES = TOKENS // P
 FLOPS = 2 * (2 * TOKENS * WIDTH * WIDTH + 2 * TOKENS * WIDTH * KEYS)
-WARM = 4
-AWAY = {(0, 1, 1), (0, 2, 1)}
+WARM = 3
 INV_SQRT = 1.0 / WIDTH**0.5
 
 
@@ -47,14 +45,15 @@ def tile_executor_pa_w8_kernel(
         xg = [sb("xg_%d" % g, [P, HALVES, P, 4], BF16) for g in range(GROUPS)]
         xq = [sb("xq_%d" % g, [P, TOKENS], U32) for g in range(GROUPS)]
         xqs = [sb("xqs_%d" % g, [P, TOKENS], U8) for g in range(GROUPS)]
-        wc = [[sb("wc_%d_%d" % (g, n), [P, GROUP], U32) for n in range(GROUPS)] if g == 0 else sb("wc_%d" % g, [P, WIDTH], U32) for g in range(GROUPS)]
+        wc = [sb("wc_%d" % g, [P, WIDTH], U32) for g in range(GROUPS)]
         wp = [sb("wp_%d" % n, [P, GROUPS, GROUP], U32) for n in range(GROUPS)]
         kc = sb("kc", [P, GROUPS, KEYS], U32)
         kp = sb("kp", [P, GROUPS, KEYS], U32)
-        wcs = sb("wcs", [P, GROUPS, WIDTH], U8)
-        wps = sb("wps", [P, GROUPS, WIDTH], U8)
-        kcs = sb("kcs", [P, GROUPS, KEYS], U8)
-        kps = sb("kps", [P, GROUPS, KEYS], U8)
+        wcs_head = sb("wcs_head", [P, WIDTH], U8)
+        wcs_rest = sb("wcs_rest", [P, WIDTH], U8)
+        wps = sb("wps", [P, WIDTH], U8)
+        kcs = sb("kcs", [P, KEYS], U8)
+        kps = sb("kps", [P, KEYS], U8)
         ident = sb("ident", [P, P], F32)
         ones = sb("ones", [P, P], BF16)
         brow = [sb("brow_%d" % q, [P, WIDTH], BF16) for q in range(2)]
@@ -68,51 +67,41 @@ def tile_executor_pa_w8_kernel(
 
         xv = x_bytes.rearrange("(t p) k -> p t k", t=HALVES)
 
-        def scales_in(dst, src, rows):
-            for r in rows:
+        def scales_in(dst, src, g0, g1, quads):
+            for q in quads:
                 nc.sync.dma_start(
-                    out=dst[r:P:32, :, :].bitcast(I32),
-                    in_=src[:, r:16:4, :].rearrange("g q n -> q g n").bitcast(I32),
+                    out=dst[32 * q : 32 * q + 4 * (g1 - g0), :].bitcast(I32), in_=src[g0:g1, 4 * q : 4 * q + 4, :].bitcast(I32)
                 )
 
         def clear(engine, t):
             engine.memset(t.bitcast(I32), 0)
 
-        def flat(t):
-            return t[:].rearrange("p g n -> p (g n)")
-
-        def load_wc(g, n=None):
-            src = wc_words[g].rearrange("p n t -> p (n t)")
-            if n is None:
-                nc.sync.dma_start(out=wc[g][:].bitcast(I32), in_=src.bitcast(I32))
-            else:
-                nc.sync.dma_start(out=wc[g][n][:].bitcast(I32), in_=src[:, 4 * n * GROUP : 4 * (n + 1) * GROUP].bitcast(I32))
+        def load_wc(g):
+            nc.sync.dma_start(out=wc[g][:].bitcast(I32), in_=wc_words[g].rearrange("p n t -> p (n t)").bitcast(I32))
 
         nc.sync.dma_start(out=x8_head[:], in_=xv[:, :, 0:GROUP])
         nc.sync.dma_start(out=x8_rest[:], in_=xv[:, :, GROUP:WIDTH])
-        nc.gpsimd.dma_start(out=xs[:], in_=x_scale.rearrange("o (g p t) -> p (o g) t", p=P, t=4))
-        clear(nc.vector, flat(wcs))
-        scales_in(wcs, wc_scales, range(4))
-        clear(nc.vector, brow[0][:])
+        nc.scalar.dma_start(out=xs[:], in_=x_scale.rearrange("o (g p t) -> p (o g) t", p=P, t=4))
+        clear(nc.gpsimd, brow[0][:])
+        nc.vector.memset(warm[:], 0.0)
+        nc.scalar.activation(warm[:], warm[:], ACT.Exp)
+        clear(nc.vector, wcs_head[:])
         nc.vector.memset(ones[:], 0.0)
         clear(nc.vector, zeros[:])
         nc.vector.memset(ones[0:1, :], 1.0)
-        clear(nc.vector, brow[1][:])
-        clear(nc.vector, flat(wps))
-        nc.vector.memset(warm[:], 0.0)
-        nc.scalar.activation(warm[:], warm[:], ACT.Exp)
-        make_identity(nc, ident[:])
-        clear(nc.gpsimd, flat(kcs))
-        nc.gpsimd.dma_start(out=brow[0][0:1, :], in_=bc.rearrange("(o n) -> o n", o=1))
-        nc.gpsimd.dma_start(out=brow[1][0:1, :], in_=bp.rearrange("(o n) -> o n", o=1))
-        clear(nc.gpsimd, flat(kps))
-        load_wc(0, 0)
-        load_wc(0, 1)
-        load_wc(0, 2)
+        clear(nc.vector, wcs_rest[:])
+        clear(nc.vector, wps[:])
+        nc.sync.dma_start(out=brow[0][0:1, :], in_=bc.rearrange("(o n) -> o n", o=1))
+        load_wc(0)
+        scales_in(wcs_head, wc_scales, 0, 1, (0, 2, 1, 3))
         load_wc(1)
-        scales_in(wps, wp_scales, (0, 1))
+        scales_in(wcs_rest, wc_scales, 1, 3, (0, 2, 1, 3))
         load_wc(2)
-        scales_in(wps, wp_scales, (2, 3))
+        clear(nc.gpsimd, brow[1][:])
+        make_identity(nc, ident[:])
+        nc.gpsimd.dma_start(out=brow[1][0:1, :], in_=bp.rearrange("(o n) -> o n", o=1))
+        clear(nc.gpsimd, kcs[:])
+        clear(nc.gpsimd, kps[:])
 
         def load_wp(n):
             nc.sync.dma_start(
@@ -120,45 +109,37 @@ def tile_executor_pa_w8_kernel(
                 in_=wp_words[:, :, n * GROUP : (n + 1) * GROUP, :].rearrange("g p n t -> p g (n t)").bitcast(I32),
             )
 
+        def load_keys(dst, src):
+            nc.sync.dma_start(out=dst[:].bitcast(I32), in_=src.rearrange("g p n t -> p g (n t)").bitcast(I32))
+
+        scales_in(wps, wp_scales, 0, 3, (0, 2))
         load_wp(0)
-        scales_in(kcs, kc_scales, (0, 1))
+        scales_in(wps, wp_scales, 0, 3, (1, 3))
         load_wp(1)
-        scales_in(kcs, kc_scales, (2, 3))
+        scales_in(kcs, kc_scales, 0, 3, (0, 2, 1, 3))
+        load_keys(kc, kc_words)
         load_wp(2)
-        scales_in(kps, kp_scales, (0, 1))
-        nc.sync.dma_start(out=kc[:].bitcast(I32), in_=kc_words.rearrange("g p n t -> p g (n t)").bitcast(I32))
-        scales_in(kps, kp_scales, (2, 3))
-        nc.sync.dma_start(out=kp[:].bitcast(I32), in_=kp_words.rearrange("g p n t -> p g (n t)").bitcast(I32))
+        scales_in(kps, kp_scales, 0, 3, (0, 2, 1, 3))
+        load_keys(kp, kp_words)
 
         def widen(engine_copy, g, t):
             engine_copy(out=xw[g][:, t, :], in_=(x8_head[:, t, :] if g == 0 else x8_rest[:, t, (g - 1) * GROUP : g * GROUP]).bitcast(FP8))
 
         def x_transposes(g, b):
-            xt = bank("xt_%d" % g, b, [P, 2, HALVES, P], F32)
+            xt = bank("xt_%d" % g, b, [P, HALVES, 2, P], F32)
             for t in range(HALVES):
                 words = xw[g][:, t, :].bitcast(F32)
                 for u in range(2):
-                    nc.tensor.transpose(xt[:, u, t, :], words[:, u : GROUP // 2 : 2], ident[:])
+                    nc.tensor.transpose(xt[:, t, u, :], words[:, u : GROUP // 2 : 2], ident[:])
             return xt
 
         def x_scaled(xt, g, t):
             nc.vector.tensor_tensor(
                 out=xg[g][:, t, :, :].rearrange("p r (u e) -> p r u e", e=2),
-                in0=xt[:, :, t, :].bitcast(BF16).rearrange("p u (r e) -> p r u e", e=2),
+                in0=xt[:, t, :, :].bitcast(BF16).rearrange("p u (r e) -> p r u e", e=2),
                 in1=xs[:, g : g + 1, :].to_broadcast([P, P, 4]).rearrange("p r (u e) -> p r u e", e=2),
                 op=ALU.mult,
             )
-
-        def x_scaled_whole(xt, g):
-            nc.vector.tensor_tensor(
-                out=xg[g][:].rearrange("p t r (u e) -> p (t r) u e", e=2),
-                in0=xt[:].rearrange("p u t r -> p u (t r)").bitcast(BF16).rearrange("p u (r e) -> p r u e", e=2),
-                in1=xs[:, g : g + 1, :].to_broadcast([P, TOKENS, 4]).rearrange("p r (u e) -> p r u e", e=2),
-                op=ALU.mult,
-            )
-
-        def x_quantize_whole(g):
-            nc.vector.quantize_mx(out=xq[g][:].bitcast(FP8X4), scales=xqs[g][:], in_=xg[g][:].rearrange("p t r j -> p (t r j)"))
 
         def x_quantize(g, t):
             cols = slice(t * P, (t + 1) * P)
@@ -171,7 +152,7 @@ def tile_executor_pa_w8_kernel(
             cols = slice(n * GROUP, (n + 1) * GROUP)
             nc.tensor.matmul_mx(
                 out=acc[:], lhsT=xq[g][:, rows].bitcast(FP8X4), lhsT_scale=xqs[g][:, rows],
-                rhs=(wc[g][n][:] if g == 0 else wc[g][:, cols]).bitcast(FP8X4), rhs_scale=wcs[:, g, cols], start=(g == 0), stop=(g == GROUPS - 1),
+                rhs=wc[g][:, cols].bitcast(FP8X4), rhs_scale=wcs_head[:, cols] if g == 0 else wcs_rest[4 * (g - 1) : P, cols], start=(g == 0), stop=(g == GROUPS - 1),
             )
 
         def pass_p(acc, g, n, t):
@@ -179,18 +160,11 @@ def tile_executor_pa_w8_kernel(
             cols = slice(n * GROUP, (n + 1) * GROUP)
             nc.tensor.matmul_mx(
                 out=acc[:], lhsT=xq[g][:, rows].bitcast(FP8X4), lhsT_scale=xqs[g][:, rows],
-                rhs=wp[n][:, g, :].bitcast(FP8X4), rhs_scale=wps[:, g, cols], start=(g == 0), stop=(g == GROUPS - 1),
+                rhs=wp[n][:, g, :].bitcast(FP8X4), rhs_scale=wps[4 * g : P, cols], start=(g == 0), stop=(g == GROUPS - 1),
             )
 
         def add_bias(acc, q, n, t):
-            if (q, n, t) in AWAY:
-                side = sb("side_%d_%d_%d" % (q, n, t), [P, GROUP], F32)
-                nc.scalar.copy(out=side[:], in_=acc[:])
-                acc = side
-                engine = nc.gpsimd
-            else:
-                engine = nc.vector
-            engine.tensor_tensor(
+            nc.vector.tensor_tensor(
                 out=qb[q][n][t][:].rearrange("p (u m e) -> p u m e", u=2, e=2),
                 in0=acc[:].rearrange("p (m u e) -> p u m e", u=2, e=2),
                 in1=bias[q][:, n * GROUP : (n + 1) * GROUP].rearrange("p (u m e) -> p u m e", u=2, e=2),
@@ -242,10 +216,10 @@ def tile_executor_pa_w8_kernel(
             k, ks = ((kc, kcs), (kp, kps))[q]
             nc.tensor.matmul_mx(
                 out=z[:], lhsT=qq[q][n][:, rows].bitcast(FP8X4), lhsT_scale=qqs[q][n][:, rows],
-                rhs=k[:, n, :].bitcast(FP8X4), rhs_scale=ks[:, n, :], start=(n == 0), stop=(n == GROUPS - 1),
+                rhs=k[:, n, :].bitcast(FP8X4), rhs_scale=ks[4 * n : P, :], start=(n == 0), stop=(n == GROUPS - 1),
             )
 
-        peak = [[sb("peak_%d_%d" % (q, t), [P, 1], F32) for t in range(HALVES)] for q in range(2)]
+        scaled = [[sb("scaled_%d_%d" % (q, t), [P, KEYS], F32) for t in range(HALVES)] for q in range(2)]
         shift = [[sb("shift_%d_%d" % (q, t), [P, 1], F32) for t in range(HALVES)] for q in range(2)]
         total = [[sb("total_%d_%d" % (q, t), [P, 1], F32) for t in range(HALVES)] for q in range(2)]
         recip = [[sb("recip_%d_%d" % (q, t), [P, 1], F32) for t in range(HALVES)] for q in range(2)]
@@ -253,18 +227,16 @@ def tile_executor_pa_w8_kernel(
         soft = [[sb("soft_%d_%d" % (q, t), [P, KEYS], F32) for t in range(HALVES)] for q in range(2)]
 
         def row_max(z, q, t):
-            nc.vector.tensor_reduce(out=peak[q][t][:], in_=z[:], axis=AXIS.X, op=ALU.max)
-            nc.vector.tensor_scalar(out=shift[q][t][:], in0=peak[q][t][:], scalar1=-INV_SQRT, scalar2=None, op0=ALU.mult)
+            nc.vector.tensor_scalar(
+                out=scaled[q][t][:], in0=z[:], scalar1=-INV_SQRT, scalar2=None, op0=ALU.mult, op1=ALU.min, accum_out=shift[q][t][:]
+            )
 
         def row_exp(z, q, t):
             nc.scalar.activation(expo[q][t][:], z[:], ACT.Exp, bias=shift[q][t][:], scale=INV_SQRT, accum_out=total[q][t][:])
 
-        def normalise(q, t, on_scalar):
+        def normalise(q, t):
             nc.vector.reciprocal(out=recip[q][t][:], in_=total[q][t][:])
-            if on_scalar:
-                nc.gpsimd.tensor_scalar(out=soft[q][t][:], in0=expo[q][t][:], scalar1=recip[q][t][:], scalar2=0.0, op0=ALU.mult, op1=ALU.add)
-            else:
-                nc.vector.tensor_scalar(out=soft[q][t][:], in0=expo[q][t][:], scalar1=recip[q][t][:], scalar2=None, op0=ALU.mult)
+            nc.vector.tensor_scalar(out=soft[q][t][:], in0=expo[q][t][:], scalar1=recip[q][t][:], scalar2=None, op0=ALU.mult)
             nc.sync.dma_start(out=(out_c, out_p)[q][t * P : (t + 1) * P, :], in_=soft[q][t][:])
 
         for i in range(WARM):
@@ -276,6 +248,14 @@ def tile_executor_pa_w8_kernel(
         widen(nc.scalar.copy, 1, 1)
         widen(nc.scalar.copy, 2, 1)
         xt0 = x_transposes(0, 0)
+        bt_c = bias_bank("bt_c", 4)
+        bt_t = bias_bank("bt_t", 6)
+        spread_bias(bt_t, 0, 0, 2)
+        for n in range(2):
+            spread_bias(bt_c, n, 0, n)
+        keep_bias(bt_t, 0, 0, 2)
+        for n in range(2):
+            keep_bias(bt_c, n, 0, n)
         x_scaled(xt0, 0, 0)
         x_quantize(0, 0)
         x_scaled(xt0, 0, 1)
@@ -287,33 +267,26 @@ def tile_executor_pa_w8_kernel(
         acc_c = {}
         for n in range(GROUPS):
             acc_c[n, 0] = bank("acc_c_%d_0" % n, (3, 5, 7)[n], [P, GROUP], F32)
-        for n in range(GROUPS):
             pass_c(acc_c[n, 0], 0, n, 0)
         xt2 = x_transposes(2, 0)
-        bt_c = bias_bank("bt_c", 2)
-        for n in range(2):
-            spread_bias(bt_c, n, 0, n)
-            keep_bias(bt_c, n, 0, n)
         for n in range(GROUPS):
             acc_c[n, 1] = bank("acc_c_%d_1" % n, (4, 6, 2)[n], [P, GROUP], F32)
             pass_c(acc_c[n, 1], 0, n, 1)
+        bt_p = bias_bank("bt_p", 1)
+        for n in range(2):
+            spread_bias(bt_p, n, 1, n)
+            keep_bias(bt_p, n, 1, n)
         x_scaled(xt2, 2, 0)
         x_quantize(1, 1)
         x_scaled(xt2, 2, 1)
         x_quantize(2, 0)
         x_quantize(2, 1)
-        for n in range(GROUPS):
-            pass_c(acc_c[n, 0], 1, n, 0)
-        bt_t = bias_bank("bt_t", 1)
-        for q in range(2):
-            spread_bias(bt_t, q, q, 2)
-            keep_bias(bt_t, q, q, 2)
-        for n in range(GROUPS):
-            pass_c(acc_c[n, 1], 1, n, 1)
-        bt_p = bias_bank("bt_p", 0)
-        for n in range(2):
-            spread_bias(bt_p, n, 1, n)
-            keep_bias(bt_p, n, 1, n)
+        for t in range(HALVES):
+            for n in range(GROUPS):
+                pass_c(acc_c[n, t], 1, n, t)
+        bt_q = bias_bank("bt_q", 0)
+        spread_bias(bt_q, 0, 1, 2)
+        keep_bias(bt_q, 0, 1, 2)
         for n in range(GROUPS):
             for t in range(HALVES):
                 pass_c(acc_c[n, t], 2, n, t)
@@ -329,47 +302,47 @@ def tile_executor_pa_w8_kernel(
             return accs
 
         acc = project_p(0, (1, 0))
-        q_empty(q_transposes(0, 0, 3), 0, 0)
-        q_empty(q_transposes(0, 1, 4), 0, 1)
+        for n in range(GROUPS):
+            q_empty(q_transposes(0, n, (3, 4, 5)[n]), 0, n)
         for t in range(HALVES):
             add_bias(acc[t], 1, 0, t)
-        q_quantize(0, 0)
-        q_quantize(0, 1)
-        acc = project_p(1, (5, 6))
-        q_empty(q_transposes(0, 2, 7), 0, 2)
-        q_empty(q_transposes(1, 0, 2), 1, 0)
+        for n in range(2):
+            q_quantize(0, n)
+        acc = project_p(1, (6, 2))
+        q_quantize(0, 2)
         for t in range(HALVES):
             add_bias(acc[t], 1, 1, t)
-        q_quantize(0, 2)
-        q_quantize(1, 0)
-        zc = [bank("zc_%d" % t, (3, 4)[t], [P, KEYS], F32) for t in range(HALVES)]
-        acc = project_p(2, (1, 0))
-        for t in range(HALVES):
-            add_bias(acc[t], 1, 2, t)
+        zc = [bank("zc_0", 7, [P, KEYS], F32)]
         for n in range(GROUPS):
             score(zc[0], 0, n, 0)
-        tb = [q_transposes(1, n, (None, 5, 6)[n]) for n in (1, 2)]
-        q_empty(tb[0], 1, 1)
-        for t in range(HALVES):
-            q_empty_half(tb[1], 1, 2, t)
+        q_empty(q_transposes(1, 0, 1), 1, 0)
+        q_empty(q_transposes(1, 1, 0), 1, 1)
         row_max(zc[0], 0, 0)
         row_exp(zc[0], 0, 0)
-        for n in range(GROUPS):
-            score(zc[1], 0, n, 1)
+        q_quantize(1, 0)
+        acc = project_p(2, (3, 4))
         q_quantize(1, 1)
         for t in range(HALVES):
-            q_quantize_half(1, 2, t)
-        zp = [bank("zp_%d" % t, (7, 2)[t], [P, KEYS], F32) for t in range(HALVES)]
+            add_bias(acc[t], 1, 2, t)
+        normalise(0, 0)
+        zc.append(bank("zc_1", 5, [P, KEYS], F32))
+        for n in range(GROUPS):
+            score(zc[1], 0, n, 1)
+        tb = q_transposes(1, 2, 6)
         for t in range(HALVES):
-            for n in range(GROUPS):
-                score(zp[t], 1, n, t)
+            q_empty_half(tb, 1, 2, t)
         row_max(zc[1], 0, 1)
         row_exp(zc[1], 0, 1)
-        normalise(0, 0, True)
+        for t in range(HALVES):
+            q_quantize_half(1, 2, t)
+        zp = [bank("zp_%d" % t, (2, 7)[t], [P, KEYS], F32) for t in range(HALVES)]
+        for n in range(GROUPS):
+            for t in range(HALVES):
+                score(zp[t], 1, n, t)
         row_max(zp[0], 1, 0)
         row_exp(zp[0], 1, 0)
         row_max(zp[1], 1, 1)
-        normalise(0, 1, True)
         row_exp(zp[1], 1, 1)
-        normalise(1, 0, False)
-        normalise(1, 1, False)
+        normalise(0, 1)
+        normalise(1, 0)
+        normalise(1, 1)

@@ -19,7 +19,7 @@ GROUP = 512
 GROUPS = WIDTH // GROUP
 HALVES = TOKENS // P
 FLOPS = 2 * (2 * TOKENS * WIDTH * WIDTH + 2 * TOKENS * WIDTH * KEYS)
-WARM = 3
+WARM = 4
 INV_SQRT = 1.0 / WIDTH**0.5
 
 
@@ -49,11 +49,11 @@ def tile_executor_pa_w8_kernel(
         wp = [sb("wp_%d" % n, [P, GROUPS, GROUP], U32) for n in range(GROUPS)]
         kc = sb("kc", [P, GROUPS, KEYS], U32)
         kp = sb("kp", [P, GROUPS, KEYS], U32)
-        wcs_head = sb("wcs_head", [P, WIDTH], U8)
-        wcs_rest = sb("wcs_rest", [P, WIDTH], U8)
-        wps = sb("wps", [P, WIDTH], U8)
-        kcs = sb("kcs", [P, KEYS], U8)
-        kps = sb("kps", [P, KEYS], U8)
+        wcs_head = sb("wcs_head", [P, 1, WIDTH], U8)
+        wcs_rest = sb("wcs_rest", [P, GROUPS - 1, WIDTH], U8)
+        wps = sb("wps", [P, GROUPS, WIDTH], U8)
+        kcs = sb("kcs", [P, GROUPS, KEYS], U8)
+        kps = sb("kps", [P, GROUPS, KEYS], U8)
         ident = sb("ident", [P, P], F32)
         ones = sb("ones", [P, P], BF16)
         brow = [sb("brow_%d" % q, [P, WIDTH], BF16) for q in range(2)]
@@ -67,14 +67,18 @@ def tile_executor_pa_w8_kernel(
 
         xv = x_bytes.rearrange("(t p) k -> p t k", t=HALVES)
 
-        def scales_in(dst, src, g0, g1, quads):
-            for q in quads:
+        def scales_in(dst, src, g0, g1):
+            for q in (0, 2, 1, 3):
                 nc.sync.dma_start(
-                    out=dst[32 * q : 32 * q + 4 * (g1 - g0), :].bitcast(I32), in_=src[g0:g1, 4 * q : 4 * q + 4, :].bitcast(I32)
+                    out=dst[32 * q : 32 * q + 4, :, :].bitcast(I32),
+                    in_=src[g0:g1, 4 * q : 4 * q + 4, :].rearrange("g r n -> r g n").bitcast(I32),
                 )
 
         def clear(engine, t):
             engine.memset(t.bitcast(I32), 0)
+
+        def flat(t):
+            return t[:].rearrange("p g n -> p (g n)")
 
         def load_wc(g):
             nc.sync.dma_start(out=wc[g][:].bitcast(I32), in_=wc_words[g].rearrange("p n t -> p (n t)").bitcast(I32))
@@ -82,26 +86,27 @@ def tile_executor_pa_w8_kernel(
         nc.sync.dma_start(out=x8_head[:], in_=xv[:, :, 0:GROUP])
         nc.sync.dma_start(out=x8_rest[:], in_=xv[:, :, GROUP:WIDTH])
         nc.scalar.dma_start(out=xs[:], in_=x_scale.rearrange("o (g p t) -> p (o g) t", p=P, t=4))
-        clear(nc.gpsimd, brow[0][:])
+        clear(nc.gpsimd, zeros[:])
+        clear(nc.gpsimd, brow[0][:, 0 : WIDTH // 2])
+        make_identity(nc, ident[:])
         nc.vector.memset(warm[:], 0.0)
         nc.scalar.activation(warm[:], warm[:], ACT.Exp)
-        clear(nc.vector, wcs_head[:])
+        clear(nc.vector, brow[0][:, WIDTH // 2 : WIDTH])
+        clear(nc.vector, flat(wcs_head))
         nc.vector.memset(ones[:], 0.0)
-        clear(nc.vector, zeros[:])
         nc.vector.memset(ones[0:1, :], 1.0)
-        clear(nc.vector, wcs_rest[:])
-        clear(nc.vector, wps[:])
+        clear(nc.vector, flat(wcs_rest))
         nc.sync.dma_start(out=brow[0][0:1, :], in_=bc.rearrange("(o n) -> o n", o=1))
         load_wc(0)
-        scales_in(wcs_head, wc_scales, 0, 1, (0, 2, 1, 3))
+        scales_in(wcs_head, wc_scales, 0, 1)
         load_wc(1)
-        scales_in(wcs_rest, wc_scales, 1, 3, (0, 2, 1, 3))
-        load_wc(2)
         clear(nc.gpsimd, brow[1][:])
-        make_identity(nc, ident[:])
-        nc.gpsimd.dma_start(out=brow[1][0:1, :], in_=bp.rearrange("(o n) -> o n", o=1))
-        clear(nc.gpsimd, kcs[:])
-        clear(nc.gpsimd, kps[:])
+        nc.sync.dma_start(out=brow[1][0:1, :], in_=bp.rearrange("(o n) -> o n", o=1))
+        scales_in(wcs_rest, wc_scales, 1, 3)
+        load_wc(2)
+        clear(nc.gpsimd, flat(wps))
+        clear(nc.gpsimd, flat(kcs))
+        clear(nc.gpsimd, flat(kps))
 
         def load_wp(n):
             nc.sync.dma_start(
@@ -112,14 +117,13 @@ def tile_executor_pa_w8_kernel(
         def load_keys(dst, src):
             nc.sync.dma_start(out=dst[:].bitcast(I32), in_=src.rearrange("g p n t -> p g (n t)").bitcast(I32))
 
-        scales_in(wps, wp_scales, 0, 3, (0, 2))
+        scales_in(wps, wp_scales, 0, 3)
         load_wp(0)
-        scales_in(wps, wp_scales, 0, 3, (1, 3))
         load_wp(1)
-        scales_in(kcs, kc_scales, 0, 3, (0, 2, 1, 3))
+        scales_in(kcs, kc_scales, 0, 3)
         load_keys(kc, kc_words)
         load_wp(2)
-        scales_in(kps, kp_scales, 0, 3, (0, 2, 1, 3))
+        scales_in(kps, kp_scales, 0, 3)
         load_keys(kp, kp_words)
 
         def widen(engine_copy, g, t):
@@ -152,7 +156,7 @@ def tile_executor_pa_w8_kernel(
             cols = slice(n * GROUP, (n + 1) * GROUP)
             nc.tensor.matmul_mx(
                 out=acc[:], lhsT=xq[g][:, rows].bitcast(FP8X4), lhsT_scale=xqs[g][:, rows],
-                rhs=wc[g][:, cols].bitcast(FP8X4), rhs_scale=wcs_head[:, cols] if g == 0 else wcs_rest[4 * (g - 1) : P, cols], start=(g == 0), stop=(g == GROUPS - 1),
+                rhs=wc[g][:, cols].bitcast(FP8X4), rhs_scale=wcs_head[:, 0, cols] if g == 0 else wcs_rest[:, g - 1, cols], start=(g == 0), stop=(g == GROUPS - 1),
             )
 
         def pass_p(acc, g, n, t):
@@ -160,7 +164,7 @@ def tile_executor_pa_w8_kernel(
             cols = slice(n * GROUP, (n + 1) * GROUP)
             nc.tensor.matmul_mx(
                 out=acc[:], lhsT=xq[g][:, rows].bitcast(FP8X4), lhsT_scale=xqs[g][:, rows],
-                rhs=wp[n][:, g, :].bitcast(FP8X4), rhs_scale=wps[4 * g : P, cols], start=(g == 0), stop=(g == GROUPS - 1),
+                rhs=wp[n][:, g, :].bitcast(FP8X4), rhs_scale=wps[:, g, cols], start=(g == 0), stop=(g == GROUPS - 1),
             )
 
         def add_bias(acc, q, n, t):
@@ -181,6 +185,14 @@ def tile_executor_pa_w8_kernel(
             nc.scalar.copy(
                 out=bias[q][:, n * GROUP : (n + 1) * GROUP].rearrange("p (u m e) -> p u m e", u=2, e=2),
                 in_=bt[:, slot, :].rearrange("p (m u e) -> p u m e", u=2, e=2),
+            )
+
+        def add_bias_word_half(acc, q, n, t, u):
+            nc.vector.tensor_tensor(
+                out=qb[q][n][t][:].rearrange("p (u m e) -> p u m e", u=2, e=2)[:, u, :, :],
+                in0=acc[:].rearrange("p (m u e) -> p u m e", u=2, e=2)[:, u, :, :],
+                in1=bias[q][:, n * GROUP : (n + 1) * GROUP].rearrange("p (u m e) -> p u m e", u=2, e=2)[:, u, :, :],
+                op=ALU.add,
             )
 
         def q_transposes(q, n, b):
@@ -216,7 +228,7 @@ def tile_executor_pa_w8_kernel(
             k, ks = ((kc, kcs), (kp, kps))[q]
             nc.tensor.matmul_mx(
                 out=z[:], lhsT=qq[q][n][:, rows].bitcast(FP8X4), lhsT_scale=qqs[q][n][:, rows],
-                rhs=k[:, n, :].bitcast(FP8X4), rhs_scale=ks[4 * n : P, :], start=(n == 0), stop=(n == GROUPS - 1),
+                rhs=k[:, n, :].bitcast(FP8X4), rhs_scale=ks[:, n, :], start=(n == 0), stop=(n == GROUPS - 1),
             )
 
         scaled = [[sb("scaled_%d_%d" % (q, t), [P, KEYS], F32) for t in range(HALVES)] for q in range(2)]
@@ -234,19 +246,29 @@ def tile_executor_pa_w8_kernel(
         def row_exp(z, q, t):
             nc.scalar.activation(expo[q][t][:], z[:], ACT.Exp, bias=shift[q][t][:], scale=INV_SQRT, accum_out=total[q][t][:])
 
-        def normalise(q, t):
+        def normalise_halves(q, t):
             nc.vector.reciprocal(out=recip[q][t][:], in_=total[q][t][:])
-            nc.vector.tensor_scalar(out=soft[q][t][:], in0=expo[q][t][:], scalar1=recip[q][t][:], scalar2=None, op0=ALU.mult)
+            for h in range(2):
+                cols = slice(h * (KEYS // 2), (h + 1) * (KEYS // 2))
+                nc.vector.tensor_scalar(out=soft[q][t][:, cols], in0=expo[q][t][:, cols], scalar1=recip[q][t][:], scalar2=None, op0=ALU.mult)
+                nc.sync.dma_start(out=(out_c, out_p)[q][t * P : (t + 1) * P, cols], in_=soft[q][t][:, cols])
+
+        def normalise(q, t, on_scalar=False):
+            nc.vector.reciprocal(out=recip[q][t][:], in_=total[q][t][:])
+            if on_scalar:
+                nc.scalar.activation(soft[q][t][:], expo[q][t][:], ACT.Copy, scale=recip[q][t][:])
+            else:
+                nc.vector.tensor_scalar(out=soft[q][t][:], in0=expo[q][t][:], scalar1=recip[q][t][:], scalar2=None, op0=ALU.mult)
             nc.sync.dma_start(out=(out_c, out_p)[q][t * P : (t + 1) * P, :], in_=soft[q][t][:])
 
         for i in range(WARM):
-            nc.tensor.matmul(bank("warm_%d" % i, 7, [P, GROUP], F32)[:], ones[:], zeros[:], start=True, stop=True)
+            nc.tensor.matmul(bank("warm_%d" % i, 7, [P, GROUP], F32)[:], zeros[:, 0:P], zeros[:], start=True, stop=True)
         widen(nc.vector.tensor_copy, 0, 0)
         widen(nc.scalar.copy, 0, 1)
         widen(nc.scalar.copy, 1, 0)
         widen(nc.vector.tensor_copy, 2, 0)
         widen(nc.scalar.copy, 1, 1)
-        widen(nc.scalar.copy, 2, 1)
+        widen(nc.vector.tensor_copy, 2, 1)
         xt0 = x_transposes(0, 0)
         bt_c = bias_bank("bt_c", 4)
         bt_t = bias_bank("bt_t", 6)
@@ -261,6 +283,7 @@ def tile_executor_pa_w8_kernel(
         x_scaled(xt0, 0, 1)
         x_quantize(0, 1)
         xt1 = x_transposes(1, 1)
+        xt2 = x_transposes(2, 2)
         x_scaled(xt1, 1, 0)
         x_scaled(xt1, 1, 1)
         x_quantize(1, 0)
@@ -268,9 +291,8 @@ def tile_executor_pa_w8_kernel(
         for n in range(GROUPS):
             acc_c[n, 0] = bank("acc_c_%d_0" % n, (3, 5, 7)[n], [P, GROUP], F32)
             pass_c(acc_c[n, 0], 0, n, 0)
-        xt2 = x_transposes(2, 0)
         for n in range(GROUPS):
-            acc_c[n, 1] = bank("acc_c_%d_1" % n, (4, 6, 2)[n], [P, GROUP], F32)
+            acc_c[n, 1] = bank("acc_c_%d_1" % n, (4, 6, 0)[n], [P, GROUP], F32)
             pass_c(acc_c[n, 1], 0, n, 1)
         bt_p = bias_bank("bt_p", 1)
         for n in range(2):
@@ -284,7 +306,7 @@ def tile_executor_pa_w8_kernel(
         for t in range(HALVES):
             for n in range(GROUPS):
                 pass_c(acc_c[n, t], 1, n, t)
-        bt_q = bias_bank("bt_q", 0)
+        bt_q = bias_bank("bt_q", 2)
         spread_bias(bt_q, 0, 1, 2)
         keep_bias(bt_q, 0, 1, 2)
         for n in range(GROUPS):
@@ -301,14 +323,14 @@ def tile_executor_pa_w8_kernel(
                 accs.append(acc)
             return accs
 
-        acc = project_p(0, (1, 0))
+        acc = project_p(0, (1, 2))
         for n in range(GROUPS):
             q_empty(q_transposes(0, n, (3, 4, 5)[n]), 0, n)
         for t in range(HALVES):
             add_bias(acc[t], 1, 0, t)
         for n in range(2):
             q_quantize(0, n)
-        acc = project_p(1, (6, 2))
+        acc = project_p(1, (6, 0))
         q_quantize(0, 2)
         for t in range(HALVES):
             add_bias(acc[t], 1, 1, t)
@@ -316,14 +338,15 @@ def tile_executor_pa_w8_kernel(
         for n in range(GROUPS):
             score(zc[0], 0, n, 0)
         q_empty(q_transposes(1, 0, 1), 1, 0)
-        q_empty(q_transposes(1, 1, 0), 1, 1)
+        q_empty(q_transposes(1, 1, 2), 1, 1)
         row_max(zc[0], 0, 0)
         row_exp(zc[0], 0, 0)
         q_quantize(1, 0)
         acc = project_p(2, (3, 4))
         q_quantize(1, 1)
-        for t in range(HALVES):
-            add_bias(acc[t], 1, 2, t)
+        add_bias(acc[0], 1, 2, 0)
+        for u in range(2):
+            add_bias_word_half(acc[1], 1, 2, 1, u)
         normalise(0, 0)
         zc.append(bank("zc_1", 5, [P, KEYS], F32))
         for n in range(GROUPS):
@@ -335,14 +358,14 @@ def tile_executor_pa_w8_kernel(
         row_exp(zc[1], 0, 1)
         for t in range(HALVES):
             q_quantize_half(1, 2, t)
-        zp = [bank("zp_%d" % t, (2, 7)[t], [P, KEYS], F32) for t in range(HALVES)]
+        zp = [bank("zp_%d" % t, (0, 7)[t], [P, KEYS], F32) for t in range(HALVES)]
         for n in range(GROUPS):
             for t in range(HALVES):
                 score(zp[t], 1, n, t)
+        normalise(0, 1, on_scalar=True)
         row_max(zp[0], 1, 0)
         row_exp(zp[0], 1, 0)
         row_max(zp[1], 1, 1)
         row_exp(zp[1], 1, 1)
-        normalise(0, 1)
         normalise(1, 0)
-        normalise(1, 1)
+        normalise_halves(1, 1)

@@ -49,11 +49,11 @@ def tile_executor_pa_w8_kernel(
         wp = [sb("wp_%d" % n, [P, GROUPS, GROUP], U32) for n in range(GROUPS)]
         kc = sb("kc", [P, GROUPS, KEYS], U32)
         kp = sb("kp", [P, GROUPS, KEYS], U32)
-        wcs_head = sb("wcs_head", [P, 1, WIDTH], U8)
-        wcs_rest = sb("wcs_rest", [P, GROUPS - 1, WIDTH], U8)
-        wps = sb("wps", [P, GROUPS, WIDTH], U8)
-        kcs = sb("kcs", [P, GROUPS, KEYS], U8)
-        kps = sb("kps", [P, GROUPS, KEYS], U8)
+        wcs_head = sb("wcs_head", [P, WIDTH], U8)
+        wcs_rest = sb("wcs_rest", [P, WIDTH], U8)
+        wps = sb("wps", [P, WIDTH], U8)
+        kcs = sb("kcs", [P, KEYS], U8)
+        kps = sb("kps", [P, KEYS], U8)
         ident = sb("ident", [P, P], F32)
         ones = sb("ones", [P, P], BF16)
         brow = [sb("brow_%d" % q, [P, WIDTH], BF16) for q in range(2)]
@@ -67,18 +67,14 @@ def tile_executor_pa_w8_kernel(
 
         xv = x_bytes.rearrange("(t p) k -> p t k", t=HALVES)
 
-        def scales_in(dst, src, g0, g1):
-            for q in (0, 2, 1, 3):
+        def scales_in(dst, src, g0, g1, quads):
+            for q in quads:
                 nc.sync.dma_start(
-                    out=dst[32 * q : 32 * q + 4, :, :].bitcast(I32),
-                    in_=src[g0:g1, 4 * q : 4 * q + 4, :].rearrange("g r n -> r g n").bitcast(I32),
+                    out=dst[32 * q : 32 * q + 4 * (g1 - g0), :].bitcast(I32), in_=src[g0:g1, 4 * q : 4 * q + 4, :].bitcast(I32)
                 )
 
         def clear(engine, t):
             engine.memset(t.bitcast(I32), 0)
-
-        def flat(t):
-            return t[:].rearrange("p g n -> p (g n)")
 
         def load_wc(g):
             nc.sync.dma_start(out=wc[g][:].bitcast(I32), in_=wc_words[g].rearrange("p n t -> p (n t)").bitcast(I32))
@@ -92,21 +88,21 @@ def tile_executor_pa_w8_kernel(
         nc.vector.memset(warm[:], 0.0)
         nc.scalar.activation(warm[:], warm[:], ACT.Exp)
         clear(nc.vector, brow[0][:, WIDTH // 2 : WIDTH])
-        clear(nc.vector, flat(wcs_head))
+        clear(nc.vector, wcs_head[:])
         nc.vector.memset(ones[:], 0.0)
         nc.vector.memset(ones[0:1, :], 1.0)
-        clear(nc.vector, flat(wcs_rest))
+        clear(nc.vector, wcs_rest[:])
+        clear(nc.vector, wps[:])
         nc.sync.dma_start(out=brow[0][0:1, :], in_=bc.rearrange("(o n) -> o n", o=1))
         load_wc(0)
-        scales_in(wcs_head, wc_scales, 0, 1)
-        load_wc(1)
+        scales_in(wcs_head, wc_scales, 0, 1, (0, 2, 1, 3))
         clear(nc.gpsimd, brow[1][:])
         nc.sync.dma_start(out=brow[1][0:1, :], in_=bp.rearrange("(o n) -> o n", o=1))
-        scales_in(wcs_rest, wc_scales, 1, 3)
+        load_wc(1)
+        scales_in(wcs_rest, wc_scales, 1, 3, (0, 2, 1, 3))
         load_wc(2)
-        clear(nc.gpsimd, flat(wps))
-        clear(nc.gpsimd, flat(kcs))
-        clear(nc.gpsimd, flat(kps))
+        clear(nc.gpsimd, kcs[:])
+        clear(nc.gpsimd, kps[:])
 
         def load_wp(n):
             nc.sync.dma_start(
@@ -117,13 +113,14 @@ def tile_executor_pa_w8_kernel(
         def load_keys(dst, src):
             nc.sync.dma_start(out=dst[:].bitcast(I32), in_=src.rearrange("g p n t -> p g (n t)").bitcast(I32))
 
-        scales_in(wps, wp_scales, 0, 3)
+        scales_in(wps, wp_scales, 0, 3, (0, 2))
         load_wp(0)
+        scales_in(wps, wp_scales, 0, 3, (1, 3))
         load_wp(1)
-        scales_in(kcs, kc_scales, 0, 3)
+        scales_in(kcs, kc_scales, 0, 3, (0, 2, 1, 3))
         load_keys(kc, kc_words)
         load_wp(2)
-        scales_in(kps, kp_scales, 0, 3)
+        scales_in(kps, kp_scales, 0, 3, (0, 2, 1, 3))
         load_keys(kp, kp_words)
 
         def widen(engine_copy, g, t):
@@ -156,7 +153,7 @@ def tile_executor_pa_w8_kernel(
             cols = slice(n * GROUP, (n + 1) * GROUP)
             nc.tensor.matmul_mx(
                 out=acc[:], lhsT=xq[g][:, rows].bitcast(FP8X4), lhsT_scale=xqs[g][:, rows],
-                rhs=wc[g][:, cols].bitcast(FP8X4), rhs_scale=wcs_head[:, 0, cols] if g == 0 else wcs_rest[:, g - 1, cols], start=(g == 0), stop=(g == GROUPS - 1),
+                rhs=wc[g][:, cols].bitcast(FP8X4), rhs_scale=wcs_head[:, cols] if g == 0 else wcs_rest[4 * (g - 1) : P, cols], start=(g == 0), stop=(g == GROUPS - 1),
             )
 
         def pass_p(acc, g, n, t):
@@ -164,7 +161,7 @@ def tile_executor_pa_w8_kernel(
             cols = slice(n * GROUP, (n + 1) * GROUP)
             nc.tensor.matmul_mx(
                 out=acc[:], lhsT=xq[g][:, rows].bitcast(FP8X4), lhsT_scale=xqs[g][:, rows],
-                rhs=wp[n][:, g, :].bitcast(FP8X4), rhs_scale=wps[:, g, cols], start=(g == 0), stop=(g == GROUPS - 1),
+                rhs=wp[n][:, g, :].bitcast(FP8X4), rhs_scale=wps[4 * g : P, cols], start=(g == 0), stop=(g == GROUPS - 1),
             )
 
         def add_bias(acc, q, n, t):
@@ -228,7 +225,7 @@ def tile_executor_pa_w8_kernel(
             k, ks = ((kc, kcs), (kp, kps))[q]
             nc.tensor.matmul_mx(
                 out=z[:], lhsT=qq[q][n][:, rows].bitcast(FP8X4), lhsT_scale=qqs[q][n][:, rows],
-                rhs=k[:, n, :].bitcast(FP8X4), rhs_scale=ks[:, n, :], start=(n == 0), stop=(n == GROUPS - 1),
+                rhs=k[:, n, :].bitcast(FP8X4), rhs_scale=ks[4 * n : P, :], start=(n == 0), stop=(n == GROUPS - 1),
             )
 
         scaled = [[sb("scaled_%d_%d" % (q, t), [P, KEYS], F32) for t in range(HALVES)] for q in range(2)]
@@ -272,32 +269,33 @@ def tile_executor_pa_w8_kernel(
         xt0 = x_transposes(0, 0)
         bt_c = bias_bank("bt_c", 4)
         bt_t = bias_bank("bt_t", 6)
-        spread_bias(bt_t, 0, 0, 2)
+        bt_p = bias_bank("bt_p", 7)
         for n in range(2):
             spread_bias(bt_c, n, 0, n)
-        keep_bias(bt_t, 0, 0, 2)
+        spread_bias(bt_t, 0, 0, 2)
+        xt1 = x_transposes(1, 1)
+        xt2 = x_transposes(2, 2)
+        spread_bias(bt_t, 1, 1, 2)
+        for n in range(2):
+            spread_bias(bt_p, n, 1, n)
         for n in range(2):
             keep_bias(bt_c, n, 0, n)
+        for q in range(2):
+            keep_bias(bt_t, q, q, 2)
+        for n in range(2):
+            keep_bias(bt_p, n, 1, n)
         x_scaled(xt0, 0, 0)
         x_quantize(0, 0)
         x_scaled(xt0, 0, 1)
         x_quantize(0, 1)
-        xt1 = x_transposes(1, 1)
-        xt2 = x_transposes(2, 2)
         x_scaled(xt1, 1, 0)
         x_scaled(xt1, 1, 1)
         x_quantize(1, 0)
         acc_c = {}
-        for n in range(GROUPS):
-            acc_c[n, 0] = bank("acc_c_%d_0" % n, (3, 5, 7)[n], [P, GROUP], F32)
-            pass_c(acc_c[n, 0], 0, n, 0)
-        for n in range(GROUPS):
-            acc_c[n, 1] = bank("acc_c_%d_1" % n, (4, 6, 0)[n], [P, GROUP], F32)
-            pass_c(acc_c[n, 1], 0, n, 1)
-        bt_p = bias_bank("bt_p", 1)
-        for n in range(2):
-            spread_bias(bt_p, n, 1, n)
-            keep_bias(bt_p, n, 1, n)
+        for t in range(HALVES):
+            for n in range(GROUPS):
+                acc_c[n, t] = bank("acc_c_%d_%d" % (n, t), ((3, 5, 0), (4, 6, 7))[t][n], [P, GROUP], F32)
+                pass_c(acc_c[n, t], 0, n, t)
         x_scaled(xt2, 2, 0)
         x_quantize(1, 1)
         x_scaled(xt2, 2, 1)
@@ -306,9 +304,6 @@ def tile_executor_pa_w8_kernel(
         for t in range(HALVES):
             for n in range(GROUPS):
                 pass_c(acc_c[n, t], 1, n, t)
-        bt_q = bias_bank("bt_q", 2)
-        spread_bias(bt_q, 0, 1, 2)
-        keep_bias(bt_q, 0, 1, 2)
         for n in range(GROUPS):
             for t in range(HALVES):
                 pass_c(acc_c[n, t], 2, n, t)

from contextlib import ExitStack

import concourse.mybir as mybir
from concourse.masks import make_identity

F32 = mybir.dt.float32
BF16 = mybir.dt.bfloat16
U32 = mybir.dt.uint32
I32 = mybir.dt.int32
U8 = mybir.dt.uint8
FP8 = mybir.dt.float8_e4m3fn
FP8X4 = mybir.dt.float8_e4m3fn_x4
ALU = mybir.AluOpType
ACT = mybir.ActivationFunctionType

TOKENS, WIDTH, KEYS = 256, 1536, 512
P = 128
GROUP = 512
GROUPS = WIDTH // GROUP
HALVES = TOKENS // P
FLOPS = 2 * (2 * TOKENS * WIDTH * WIDTH + 2 * TOKENS * WIDTH * KEYS)
WARM = 4
INV_SQRT = 1.0 / WIDTH**0.5


def tile_executor_pa_w8_kernel(
    tc, x_bytes, x_scale, wc_words, wc_scales, bc, wp_words, wp_scales, bp, kc_words, kc_scales, kp_words, kp_scales, out_c, out_p
):
    nc = tc.nc
    with ExitStack() as ctx:
        keep = ctx.enter_context(tc.tile_pool(name="keep", bufs=1))
        psum = ctx.enter_context(tc.psum_pool(name="psum", bufs=1))
        ctx.enter_context(tc.manual_schedule())

        def sb(name, shape, dtype):
            return keep.tile(shape, dtype, name=name, tag=name, align_bytes=256)

        def bank(name, which, shape, dtype):
            return psum.tile(shape, dtype, name=name, tag="bank%d" % which)

        x8_head = sb("x8_head", [P, HALVES, GROUP], U8)
        x8_rest = sb("x8_rest", [P, HALVES, WIDTH - GROUP], U8)
        xw = [sb("xw_%d" % g, [P, HALVES, GROUP], BF16) for g in range(GROUPS)]
        xs = sb("xs", [P, GROUPS, 4], F32)
        xg = [sb("xg_%d" % g, [P, HALVES, P, 4], BF16) for g in range(GROUPS)]
        xq = [sb("xq_%d" % g, [P, TOKENS], U32) for g in range(GROUPS)]
        xqs = [sb("xqs_%d" % g, [P, TOKENS], U8) for g in range(GROUPS)]
        wc = [sb("wc_%d" % g, [P, WIDTH], U32) for g in range(GROUPS)]
        wp = [sb("wp_%d" % n, [P, GROUPS, GROUP], U32) for n in range(GROUPS)]
        kc = sb("kc", [P, GROUPS, KEYS], U32)
        kp = sb("kp", [P, GROUPS, KEYS], U32)
        wcs_head = sb("wcs_head", [P, WIDTH], U8)
        wcs_rest = sb("wcs_rest", [P, WIDTH], U8)
        wps = sb("wps", [P, WIDTH], U8)
        kcs = sb("kcs", [P, KEYS], U8)
        kps = sb("kps", [P, KEYS], U8)
        ident = sb("ident", [P, P], F32)
        ones = sb("ones", [P, P], BF16)
        brow = [sb("brow_%d" % q, [P, WIDTH], BF16) for q in range(2)]
        bias = [sb("bias_%d" % q, [P, WIDTH], BF16) for q in range(2)]
        qb = [[[sb("qb_%d_%d_%d" % (q, n, t), [P, GROUP], BF16) for t in range(HALVES)] for n in range(GROUPS)] for q in range(2)]
        qt = [[sb("qt_%d_%d" % (q, n), [P, TOKENS, 2], F32) for n in range(GROUPS)] for q in range(2)]
        qq = [[sb("qq_%d_%d" % (q, n), [P, TOKENS], U32) for n in range(GROUPS)] for q in range(2)]
        qqs = [[sb("qqs_%d_%d" % (q, n), [P, TOKENS], U8) for n in range(GROUPS)] for q in range(2)]
        warm = sb("warm", [P, 1], F32)
        zeros = sb("zeros", [P, GROUP], BF16)

        xv = x_bytes.rearrange("(t p) k -> p t k", t=HALVES)

        def scales_in(dst, src, g0, g1, quads):
            for q in quads:
                nc.sync.dma_start(
                    out=dst[32 * q : 32 * q + 4 * (g1 - g0), :].bitcast(I32), in_=src[g0:g1, 4 * q : 4 * q + 4, :].bitcast(I32)
                )

        def clear(engine, t):
            engine.memset(t.bitcast(I32), 0)

        def load_wc(g):
            nc.sync.dma_start(out=wc[g][:].bitcast(I32), in_=wc_words[g].rearrange("p n t -> p (n t)").bitcast(I32))

        nc.sync.dma_start(out=x8_head[:], in_=xv[:, :, 0:GROUP])
        nc.sync.dma_start(out=x8_rest[:], in_=xv[:, :, GROUP:WIDTH])
        nc.scalar.dma_start(out=xs[:], in_=x_scale.rearrange("o (g p t) -> p (o g) t", p=P, t=4))
        clear(nc.gpsimd, zeros[:])
        clear(nc.gpsimd, brow[0][:, 0 : WIDTH // 2])
        make_identity(nc, ident[:])
        nc.vector.memset(warm[:], 0.0)
        nc.scalar.activation(warm[:], warm[:], ACT.Exp)
        clear(nc.vector, brow[0][:, WIDTH // 2 : WIDTH])
        clear(nc.vector, wcs_head[:])
        nc.vector.memset(ones[:], 0.0)
        nc.vector.memset(ones[0:1, :], 1.0)
        clear(nc.vector, wcs_rest[:])
        clear(nc.vector, wps[:])
        nc.sync.dma_start(out=brow[0][0:1, :], in_=bc.rearrange("(o n) -> o n", o=1))
        load_wc(0)
        scales_in(wcs_head, wc_scales, 0, 1, (0, 2, 1, 3))
        clear(nc.gpsimd, brow[1][:])
        nc.sync.dma_start(out=brow[1][0:1, :], in_=bp.rearrange("(o n) -> o n", o=1))
        load_wc(1)
        scales_in(wcs_rest, wc_scales, 1, 3, (0, 2, 1, 3))
        load_wc(2)
        clear(nc.gpsimd, kcs[:])
        clear(nc.gpsimd, kps[:])

        def load_wp(n):
            nc.sync.dma_start(
                out=wp[n][:].bitcast(I32),
                in_=wp_words[:, :, n * GROUP : (n + 1) * GROUP, :].rearrange("g p n t -> p g (n t)").bitcast(I32),
            )

        def load_keys(dst, src):
            nc.sync.dma_start(out=dst[:].bitcast(I32), in_=src.rearrange("g p n t -> p g (n t)").bitcast(I32))

        scales_in(wps, wp_scales, 0, 3, (0, 2))
        load_wp(0)
        scales_in(wps, wp_scales, 0, 3, (1, 3))
        load_wp(1)
        scales_in(kcs, kc_scales, 0, 3, (0, 2, 1, 3))
        load_keys(kc, kc_words)
        load_wp(2)
        scales_in(kps, kp_scales, 0, 3, (0, 2, 1, 3))
        load_keys(kp, kp_words)

        def widen(engine_copy, g, t):
            engine_copy(out=xw[g][:, t, :], in_=(x8_head[:, t, :] if g == 0 else x8_rest[:, t, (g - 1) * GROUP : g * GROUP]).bitcast(FP8))

        def x_transposes(g, b):
            xt = bank("xt_%d" % g, b, [P, HALVES, 2, P], F32)
            for t in range(HALVES):
                words = xw[g][:, t, :].bitcast(F32)
                for u in range(2):
                    nc.tensor.transpose(xt[:, t, u, :], words[:, u : GROUP // 2 : 2], ident[:])
            return xt

        def x_scaled(xt, g, t):
            nc.vector.tensor_tensor(
                out=xg[g][:, t, :, :].rearrange("p r (u e) -> p r u e", e=2),
                in0=xt[:, t, :, :].bitcast(BF16).rearrange("p u (r e) -> p r u e", e=2),
                in1=xs[:, g : g + 1, :].to_broadcast([P, P, 4]).rearrange("p r (u e) -> p r u e", e=2),
                op=ALU.mult,
            )

        def x_quantize(g, t):
            cols = slice(t * P, (t + 1) * P)
            nc.vector.quantize_mx(
                out=xq[g][:, cols].bitcast(FP8X4), scales=xqs[g][:, cols], in_=xg[g][:, t, :, :].rearrange("p r j -> p (r j)")
            )

        def pass_c(acc, g, n, t):
            rows = slice(t * P, (t + 1) * P)
            cols = slice(n * GROUP, (n + 1) * GROUP)
            nc.tensor.matmul_mx(
                out=acc[:], lhsT=xq[g][:, rows].bitcast(FP8X4), lhsT_scale=xqs[g][:, rows],
                rhs=wc[g][:, cols].bitcast(FP8X4), rhs_scale=wcs_head[:, cols] if g == 0 else wcs_rest[4 * (g - 1) : P, cols], start=(g == 0), stop=(g == GROUPS - 1),
            )

        def pass_p(acc, g, n, t):
            rows = slice(t * P, (t + 1) * P)
            cols = slice(n * GROUP, (n + 1) * GROUP)
            nc.tensor.matmul_mx(
                out=acc[:], lhsT=xq[g][:, rows].bitcast(FP8X4), lhsT_scale=xqs[g][:, rows],
                rhs=wp[n][:, g, :].bitcast(FP8X4), rhs_scale=wps[4 * g : P, cols], start=(g == 0), stop=(g == GROUPS - 1),
            )

        def add_bias(acc, q, n, t):
            nc.vector.tensor_tensor(
                out=qb[q][n][t][:].rearrange("p (u m e) -> p u m e", u=2, e=2),
                in0=acc[:].rearrange("p (m u e) -> p u m e", u=2, e=2),
                in1=bias[q][:, n * GROUP : (n + 1) * GROUP].rearrange("p (u m e) -> p u m e", u=2, e=2),
                op=ALU.add,
            )

        def bias_bank(name, b):
            return bank(name, b, [P, 2, GROUP], BF16)

        def spread_bias(bt, slot, q, n):
            nc.tensor.matmul(bt[:, slot, :], ones[:], brow[q][:, n * GROUP : (n + 1) * GROUP], start=True, stop=True)

        def keep_bias(bt, slot, q, n):
            nc.scalar.copy(
                out=bias[q][:, n * GROUP : (n + 1) * GROUP].rearrange("p (u m e) -> p u m e", u=2, e=2),
                in_=bt[:, slot, :].rearrange("p (m u e) -> p u m e", u=2, e=2),
            )

        def add_bias_word_half(acc, q, n, t, u):
            nc.vector.tensor_tensor(
                out=qb[q][n][t][:].rearrange("p (u m e) -> p u m e", u=2, e=2)[:, u, :, :],
                in0=acc[:].rearrange("p (m u e) -> p u m e", u=2, e=2)[:, u, :, :],
                in1=bias[q][:, n * GROUP : (n + 1) * GROUP].rearrange("p (u m e) -> p u m e", u=2, e=2)[:, u, :, :],
                op=ALU.add,
            )

        def q_transposes(q, n, b):
            tb = bank("tb_%d_%d" % (q, n), b, [P, 2, TOKENS], F32)
            for t in range(HALVES):
                words = qb[q][n][t][:].bitcast(F32)
                for u in range(2):
                    nc.tensor.transpose(tb[:, u, t * P : (t + 1) * P], words[:, u * P : (u + 1) * P], ident[:])
            return tb

        def q_empty(tb, q, n):
            nc.scalar.copy(out=qt[q][n][:], in_=tb[:].rearrange("p u r -> p r u"))

        def q_empty_half(tb, q, n, t):
            rows = slice(t * P, (t + 1) * P)
            nc.scalar.copy(out=qt[q][n][:, rows, :], in_=tb[:, :, rows].rearrange("p u r -> p r u"))

        def q_quantize_half(q, n, t):
            rows = slice(t * P, (t + 1) * P)
            nc.vector.quantize_mx(
                out=qq[q][n][:, rows].bitcast(FP8X4),
                scales=qqs[q][n][:, rows],
                in_=qt[q][n][:, rows, :].rearrange("p r u -> p (r u)").bitcast(BF16),
            )

        def q_quantize(q, n):
            nc.vector.quantize_mx(
                out=qq[q][n][:].bitcast(FP8X4), scales=qqs[q][n][:], in_=qt[q][n][:].rearrange("p r u -> p (r u)").bitcast(BF16)
            )

        def score(z, q, n, t):
            rows = slice(t * P, (t + 1) * P)
            k, ks = ((kc, kcs), (kp, kps))[q]
            nc.tensor.matmul_mx(
                out=z[:], lhsT=qq[q][n][:, rows].bitcast(FP8X4), lhsT_scale=qqs[q][n][:, rows],
                rhs=k[:, n, :].bitcast(FP8X4), rhs_scale=ks[4 * n : P, :], start=(n == 0), stop=(n == GROUPS - 1),
            )

        scaled = [[sb("scaled_%d_%d" % (q, t), [P, KEYS], F32) for t in range(HALVES)] for q in range(2)]
        shift = [[sb("shift_%d_%d" % (q, t), [P, 1], F32) for t in range(HALVES)] for q in range(2)]
        total = [[sb("total_%d_%d" % (q, t), [P, 1], F32) for t in range(HALVES)] for q in range(2)]
        recip = [[sb("recip_%d_%d" % (q, t), [P, 1], F32) for t in range(HALVES)] for q in range(2)]
        expo = [[sb("expo_%d_%d" % (q, t), [P, KEYS], F32) for t in range(HALVES)] for q in range(2)]
        soft = [[sb("soft_%d_%d" % (q, t), [P, KEYS], F32) for t in range(HALVES)] for q in range(2)]

        def row_max(z, q, t):
            nc.vector.tensor_scalar(
                out=scaled[q][t][:], in0=z[:], scalar1=-INV_SQRT, scalar2=None, op0=ALU.mult, op1=ALU.min, accum_out=shift[q][t][:]
            )

        def row_exp(z, q, t):
            nc.scalar.activation(expo[q][t][:], z[:], ACT.Exp, bias=shift[q][t][:], scale=INV_SQRT, accum_out=total[q][t][:])

        def normalise_halves(q, t):
            nc.vector.reciprocal(out=recip[q][t][:], in_=total[q][t][:])
            for h in range(2):
                cols = slice(h * (KEYS // 2), (h + 1) * (KEYS // 2))
                nc.vector.tensor_scalar(out=soft[q][t][:, cols], in0=expo[q][t][:, cols], scalar1=recip[q][t][:], scalar2=None, op0=ALU.mult)
                nc.sync.dma_start(out=(out_c, out_p)[q][t * P : (t + 1) * P, cols], in_=soft[q][t][:, cols])

        def normalise(q, t, on_scalar=False):
            nc.vector.reciprocal(out=recip[q][t][:], in_=total[q][t][:])
            if on_scalar:
                nc.scalar.activation(soft[q][t][:], expo[q][t][:], ACT.Copy, scale=recip[q][t][:])
            else:
                nc.vector.tensor_scalar(out=soft[q][t][:], in0=expo[q][t][:], scalar1=recip[q][t][:], scalar2=None, op0=ALU.mult)
            nc.sync.dma_start(out=(out_c, out_p)[q][t * P : (t + 1) * P, :], in_=soft[q][t][:])

        for i in range(WARM):
            nc.tensor.matmul(bank("warm_%d" % i, 7, [P, GROUP], F32)[:], zeros[:, 0:P], zeros[:], start=True, stop=True)
        widen(nc.vector.tensor_copy, 0, 0)
        widen(nc.scalar.copy, 0, 1)
        widen(nc.scalar.copy, 1, 0)
        widen(nc.vector.tensor_copy, 2, 0)
        widen(nc.scalar.copy, 1, 1)
        widen(nc.vector.tensor_copy, 2, 1)
        xt0 = x_transposes(0, 0)
        bt_c = bias_bank("bt_c", 4)
        bt_t = bias_bank("bt_t", 6)
        bt_p = bias_bank("bt_p", 7)
        for n in range(2):
            spread_bias(bt_c, n, 0, n)
        spread_bias(bt_t, 0, 0, 2)
        xt1 = x_transposes(1, 1)
        xt2 = x_transposes(2, 2)
        spread_bias(bt_t, 1, 1, 2)
        for n in range(2):
            spread_bias(bt_p, n, 1, n)
        for n in range(2):
            keep_bias(bt_c, n, 0, n)
        for q in range(2):
            keep_bias(bt_t, q, q, 2)
        for n in range(2):
            keep_bias(bt_p, n, 1, n)
        x_scaled(xt0, 0, 0)
        x_quantize(0, 0)
        x_scaled(xt0, 0, 1)
        x_quantize(0, 1)
        x_scaled(xt1, 1, 0)
        x_scaled(xt1, 1, 1)
        x_quantize(1, 0)
        acc_c = {}
        for t in range(HALVES):
            for n in range(GROUPS):
                acc_c[n, t] = bank("acc_c_%d_%d" % (n, t), ((3, 5, 0), (4, 6, 7))[t][n], [P, GROUP], F32)
                pass_c(acc_c[n, t], 0, n, t)
        x_scaled(xt2, 2, 0)
        x_quantize(1, 1)
        x_scaled(xt2, 2, 1)
        x_quantize(2, 0)
        x_quantize(2, 1)
        for t in range(HALVES):
            for n in range(GROUPS):
                pass_c(acc_c[n, t], 1, n, t)
        for n in range(GROUPS):
            for t in range(HALVES):
                pass_c(acc_c[n, t], 2, n, t)
                add_bias(acc_c[n, t], 0, n, t)

        def project_p(n, banks):
            accs = []
            for t in range(HALVES):
                acc = bank("acc_p_%d_%d" % (n, t), banks[t], [P, GROUP], F32)
                for g in range(GROUPS):
                    pass_p(acc, g, n, t)
                accs.append(acc)
            return accs

        acc = project_p(0, (1, 2))
        for n in range(GROUPS):
            q_empty(q_transposes(0, n, (3, 4, 5)[n]), 0, n)
        for t in range(HALVES):
            add_bias(acc[t], 1, 0, t)
        for n in range(2):
            q_quantize(0, n)
        acc = project_p(1, (6, 0))
        q_quantize(0, 2)
        for t in range(HALVES):
            add_bias(acc[t], 1, 1, t)
        zc = [bank("zc_0", 7, [P, KEYS], F32)]
        for n in range(GROUPS):
            score(zc[0], 0, n, 0)
        q_empty(q_transposes(1, 0, 1), 1, 0)
        q_empty(q_transposes(1, 1, 2), 1, 1)
        row_max(zc[0], 0, 0)
        row_exp(zc[0], 0, 0)
        q_quantize(1, 0)
        acc = project_p(2, (3, 4))
        q_quantize(1, 1)
        add_bias(acc[0], 1, 2, 0)
        for u in range(2):
            add_bias_word_half(acc[1], 1, 2, 1, u)
        normalise(0, 0)
        zc.append(bank("zc_1", 5, [P, KEYS], F32))
        for n in range(GROUPS):
            score(zc[1], 0, n, 1)
        tb = q_transposes(1, 2, 6)
        for t in range(HALVES):
            q_empty_half(tb, 1, 2, t)
        row_max(zc[1], 0, 1)
        row_exp(zc[1], 0, 1)
        for t in range(HALVES):
            q_quantize_half(1, 2, t)
        zp = [bank("zp_%d" % t, (0, 7)[t], [P, KEYS], F32) for t in range(HALVES)]
        for n in range(GROUPS):
            for t in range(HALVES):
                score(zp[t], 1, n, t)
        normalise(0, 1, on_scalar=True)
        row_max(zp[0], 1, 0)
        row_exp(zp[0], 1, 0)
        row_max(zp[1], 1, 1)
        row_exp(zp[1], 1, 1)
        normalise(1, 0)
        normalise_halves(1, 1)
